import numpy as np
import ml_dtypes


def mxq(x, axis, fmt="e4m3"):
    dtype, down = {"e4m3": (ml_dtypes.float8_e4m3fn, 7), "e5m2": (ml_dtypes.float8_e5m2, 14)}[fmt]
    v = np.moveaxis(np.asarray(x, np.float32).astype(ml_dtypes.bfloat16).astype(np.float64), axis, -1)
    blocks = v.reshape(v.shape[:-1] + (-1, 32))
    amax = np.abs(blocks).max(-1, keepdims=True)
    byte = np.maximum(np.where(amax > 0, np.frexp(amax)[1] - 1 + 127, 0) - down, 1)
    scale = np.exp2(byte - 127.0)
    codes = (blocks / scale).astype(np.float32).astype(dtype).astype(np.float64)
    return np.moveaxis((codes * scale).reshape(v.shape), -1, axis)


WIDE = False


def mx_kscale(k):
    if not WIDE:
        return np.ones(k)
    levels = np.array([10, -10, 5, -5, 0])
    if k % 512:
        return np.exp2(np.random.permutation(np.resize(levels, k // 32))).repeat(32)
    a = np.empty((k // 512, 16))
    for p in range(k // 512):
        a[p, :8] = np.random.permutation(np.resize(levels, 8))
        for g in range(8):
            far = levels[np.abs(levels - a[p, g]) >= 10]
            a[p, g + 8] = far[np.random.randint(len(far))]
    return np.exp2(a.ravel()).repeat(32)


BF16 = ml_dtypes.bfloat16


def bf(x):
    return np.asarray(x, np.float32).astype(BF16)


def f64(x):
    return np.asarray(x).astype(np.float64)


B, L, S, D, DA, H, MLP = 2, 3, 256, 1024, 1024, 16, 4096
EPS = 1e-5


def layer_norm(u, g, b):
    mu = u.mean(-1, keepdims=True)
    var = ((u - mu) ** 2).mean(-1, keepdims=True)
    return (u - mu) / np.sqrt(var + EPS) * g + b


def setup_inputs():
    s = mx_kscale(DA)
    r = np.random.standard_normal
    return {"h_attn": bf(r((B, S, DA)) * 2.0 * s), "x": bf(r((B, S, D))),
            "attn_out_W": bf(r((DA, D)) * 0.5 / np.sqrt(DA) / s[:, None]), "attn_out_b": bf(r(D) * 0.2),
            "attn_norm_g": bf(1.0 + 0.1 * r(D)), "attn_norm_b": bf(r(D) * 0.1)}


def core(h_attn, x, attn_out_W, attn_out_b, attn_norm_g, attn_norm_b):
    o = (mxq(f64(h_attn), 2, "e4m3") @ mxq(f64(attn_out_W), 0, "e4m3")) + f64(attn_out_b)
    return f64(x) + layer_norm(o, f64(attn_norm_g), f64(attn_norm_b))


def e4m3fn_bytes(y):
    return np.clip(np.asarray(y, np.float64), -448.0, 448.0).astype(np.float32).astype(ml_dtypes.float8_e4m3fn).view(np.uint8)


def reference(h_attn, x, attn_out_W, attn_out_b, attn_norm_g, attn_norm_b):
    out = core(h_attn, x, attn_out_W, attn_out_b, attn_norm_g, attn_norm_b)
    s = np.max(np.abs(out)) / 448.0
    return out, e4m3fn_bytes(out / s)

@@ -1,0 +1,234 @@
+from contextlib import ExitStack
+
+import concourse.masks as masks
+import concourse.mybir as mybir
+
+F32 = mybir.dt.float32
+BF16 = mybir.dt.bfloat16
+U32 = mybir.dt.uint32
+U8 = mybir.dt.uint8
+FP8X4 = mybir.dt.float8_e4m3fn_x4
+FP8 = mybir.dt.float8_e4m3fn
+ALU = mybir.AluOpType
+ACT = mybir.ActivationFunctionType
+AX = mybir.AxisListType
+
+P = 128
+TOK = 512
+K = 1024
+N = 1024
+MT = TOK // P
+PACK = 4
+KP = P * PACK
+G = K // KP
+NH = 512
+J = N // NH
+EPS = 1e-5
+FLOPS = 2 * TOK * K * N
+
+V_SHARE = 256
+V_CAST = 672
+
+
+def tile_dcadecoderblock_pb_kernel(tc, h_attn, x, attn_out_W, attn_out_b, attn_norm_g, attn_norm_b, out_0, out_1):
+    nc = tc.nc
+    hv = h_attn.flatten_outer_dims().rearrange("(p m) k -> p m k", m=MT)
+    xv = x.flatten_outer_dims().rearrange("(p m) n -> p m n", m=MT)
+    o0v = out_0.flatten_outer_dims().rearrange("(p m) n -> p m n", m=MT)
+    o1v = out_1.flatten_outer_dims().rearrange("(p m) n -> p m n", m=MT)
+
+    with ExitStack() as ctx:
+        sb = ctx.enter_context(tc.tile_pool(name="sb", bufs=1))
+        ps = ctx.enter_context(tc.psum_pool(name="ps", bufs=8))
+
+        one = sb.tile([P, 1], F32, name="one")
+        nc.vector.memset(one[:], 1.0)
+        zero = sb.tile([P, 1], F32, name="zero")
+        nc.vector.memset(zero[:], 0.0)
+        warm = sb.tile([P, 1], F32, name="warm")
+        nc.scalar.activation(out=warm[:], in_=one[:], func=ACT.Sqrt)
+        ident = sb.tile([P, P], F32, name="ident")
+        masks.make_identity(nc, ident[:])
+
+        chunks = [(g, j) for g in range(G) for j in range(J)]
+        w_raw = {}
+        h_sb = {}
+
+        def load_w(c):
+            g, j = c
+            t = sb.tile([P, PACK, NH], BF16, name="wraw%d%d" % c)
+            nc.sync.dma_start(
+                out=t[:],
+                in_=attn_out_W[g * KP : (g + 1) * KP, j * NH : (j + 1) * NH].rearrange("(p t) n -> p t n", t=PACK),
+            )
+            w_raw[c] = t
+
+        def load_h(m):
+            t = sb.tile([P, K], BF16, name="hsb%d" % m)
+            nc.sync.dma_start(out=t[:], in_=hv[:, m, :])
+            h_sb[m] = t
+
+        load_w(chunks[0])
+        load_h(0)
+        load_h(1)
+        load_w(chunks[1])
+        load_h(2)
+        load_h(3)
+        load_w(chunks[2])
+        load_w(chunks[3])
+        b_bc = sb.tile([P, N], BF16, name="b_bc")
+        nc.sync.dma_start(out=b_bc[:], in_=attn_out_b.partition_broadcast(P))
+        g_bc = sb.tile([P, N], BF16, name="g_bc")
+        nc.sync.dma_start(out=g_bc[:], in_=attn_norm_g.partition_broadcast(P))
+        be_bc = sb.tile([P, N], BF16, name="be_bc")
+        nc.sync.dma_start(out=be_bc[:], in_=attn_norm_b.partition_broadcast(P))
+        x_sb = {}
+        for m in range(MT):
+            t = sb.tile([P, N], BF16, name="xsb%d" % m)
+            nc.sync.dma_start(out=t[:], in_=xv[:, m, :])
+            x_sb[m] = t
+
+        w_grp = {}
+        w_codes = {}
+        w_scales = {}
+        h_grp = {}
+        h_codes = {}
+        h_scales = {}
+        acc = {}
+
+        def interleave_w(c):
+            grp = sb.tile([P, NH * PACK], BF16, name="wgrp%d%d" % c, align_bytes=64)
+            g3 = grp[:].rearrange("p (n t) -> p n t", t=PACK)
+            raw = w_raw[c]
+            nc.vector.tensor_copy(out=g3[:, 0:V_SHARE, :], in_=raw[:, :, 0:V_SHARE].rearrange("p t n -> p n t"))
+            nc.scalar.copy(out=g3[:, V_SHARE:NH, :], in_=raw[:, :, V_SHARE:NH].rearrange("p t n -> p n t"))
+            w_grp[c] = grp
+
+        def quantize_w(c):
+            codes = sb.tile([P, NH], U32, name="wc%d%d" % c, align_bytes=64)
+            scales = sb.tile([P, NH], U8, name="ws%d%d" % c, align_bytes=64)
+            nc.vector.quantize_mx(out=codes[:].bitcast(FP8X4), scales=scales[:], in_=w_grp[c][:])
+            w_codes[c] = codes
+            w_scales[c] = scales
+
+        def transpose_h(m):
+            words = h_sb[m][:].bitcast(F32)
+            xt = ps.tile([P, G, 2, P], F32, name="xt%d" % m, tag="bank")
+            for g in range(G):
+                for u in range(2):
+                    nc.tensor.transpose(xt[:, g, u, :], words[:, 256 * g + u : 256 * (g + 1) : 2], ident[:])
+            grp = sb.tile([P, G * P * PACK], BF16, name="hgrp%d" % m, align_bytes=64)
+            nc.scalar.copy(
+                out=grp[:].bitcast(F32).rearrange("p (g r u) -> p g r u", g=G, u=2),
+                in_=xt[:].rearrange("p g u r -> p g r u"),
+            )
+            h_grp[m] = grp
+
+        def quantize_h(m):
+            codes = sb.tile([P, G * P], U32, name="hc%d" % m, align_bytes=64)
+            scales = sb.tile([P, G * P], U8, name="hs%d" % m, align_bytes=64)
+            nc.vector.quantize_mx(out=codes[:].bitcast(FP8X4), scales=scales[:], in_=h_grp[m][:])
+            h_codes[m] = codes
+            h_scales[m] = scales
+
+        def mx(c, m):
+            g, j = c
+            if g == 0:
+                acc[(m, j)] = ps.tile([P, NH], F32, name="acc%d%d" % (m, j), tag="bank")
+            nc.tensor.matmul_mx(
+                out=acc[(m, j)][:],
+                lhsT=h_codes[m][:, g * P : (g + 1) * P].bitcast(FP8X4),
+                lhsT_scale=h_scales[m][:, g * P : (g + 1) * P],
+                rhs=w_codes[c][:].bitcast(FP8X4),
+                rhs_scale=w_scales[c][:],
+                start=(g == 0),
+                stop=(g == G - 1),
+            )
+
+        interleave_w(chunks[0])
+        transpose_h(0)
+        transpose_h(1)
+        interleave_w(chunks[1])
+        quantize_w(chunks[0])
+        quantize_h(0)
+        quantize_h(1)
+        transpose_h(2)
+        transpose_h(3)
+        mx(chunks[0], 0)
+        mx(chunks[0], 1)
+        interleave_w(chunks[2])
+        quantize_w(chunks[1])
+        quantize_h(2)
+        quantize_h(3)
+        mx(chunks[0], 2)
+        mx(chunks[0], 3)
+        for m in range(MT):
+            mx(chunks[1], m)
+        interleave_w(chunks[3])
+        quantize_w(chunks[2])
+        for m in range(MT):
+            mx(chunks[2], m)
+        quantize_w(chunks[3])
+        for m in range(MT):
+            mx(chunks[3], m)
+
+        am = sb.tile([P, MT], F32, name="am")
+        res = {}
+        for m in range(MT):
+            o = sb.tile([P, N], F32, name="o%d" % m)
+            sums = sb.tile([P, J], F32, name="sums%d" % m)
+            for j in range(J):
+                nc.vector.scalar_tensor_tensor(
+                    out=o[:, j * NH : (j + 1) * NH],
+                    in0=acc[(m, j)][:],
+                    scalar=1.0,
+                    in1=b_bc[:, j * NH : (j + 1) * NH],
+                    op0=ALU.mult,
+                    op1=ALU.add,
+                    accum_out=sums[:, j : j + 1],
+                )
+            negmu = sb.tile([P, 1], F32, name="negmu%d" % m)
+            nc.vector.tensor_scalar(
+                out=negmu[:], in0=sums[:, 0:1], scalar1=sums[:, 1:2], scalar2=-1.0 / N, op0=ALU.add, op1=ALU.mult
+            )
+            junk = sb.tile([P, N], BF16, name="junk%d" % m)
+            ssq = sb.tile([P, 1], F32, name="ssq%d" % m)
+            nc.scalar.activation(out=junk[:], in_=o[:], func=ACT.Square, bias=negmu[:, 0:1], scale=1.0, accum_out=ssq[:])
+            std = sb.tile([P, 1], F32, name="std%d" % m)
+            nc.scalar.activation(out=std[:], in_=ssq[:], func=ACT.Sqrt, bias=EPS, scale=1.0 / N)
+            t = sb.tile([P, N], F32, name="t%d" % m)
+            nc.vector.scalar_tensor_tensor(
+                out=t[:], in0=o[:], scalar=negmu[:, 0:1], in1=g_bc[:], op0=ALU.add, op1=ALU.mult
+            )
+            xb = sb.tile([P, N], F32, name="xb%d" % m)
+            nc.vector.tensor_tensor(out=xb[:], in0=x_sb[m][:], in1=be_bc[:], op=ALU.add)
+            rstd = sb.tile([P, 1], F32, name="rstd%d" % m)
+            nc.vector.reciprocal(out=rstd[:], in_=std[:])
+            r = sb.tile([P, N], F32, name="res%d" % m)
+            nc.vector.scalar_tensor_tensor(
+                out=r[:], in0=t[:], scalar=rstd[:, 0:1], in1=xb[:], op0=ALU.mult, op1=ALU.add
+            )
+            nc.sync.dma_start(out=o0v[:, m, :], in_=r[:])
+            nc.vector.tensor_reduce(out=am[:, m : m + 1], in_=r[:], axis=AX.X, op=ALU.max, apply_absolute_value=True)
+            res[m] = r
+
+        pm = sb.tile([P, 1], F32, name="pm")
+        nc.vector.tensor_reduce(out=pm[:], in_=am[:], axis=AX.X, op=ALU.max)
+        bt = ps.tile([P, P], F32, name="bt", tag="bank")
+        nc.tensor.transpose(bt[:], pm[:, 0:1].to_broadcast([P, P]), ident[:])
+        gm = sb.tile([P, 1], F32, name="gm")
+        nc.vector.tensor_reduce(out=gm[:], in_=bt[:], axis=AX.X, op=ALU.max)
+        rg = sb.tile([P, 1], F32, name="rg")
+        nc.vector.reciprocal(out=rg[:], in_=gm[:])
+        fac = sb.tile([P, 1], F32, name="fac")
+        nc.vector.tensor_scalar(out=fac[:], in0=rg[:], scalar1=448.0, scalar2=None, op0=ALU.mult)
+
+        for m in range(MT):
+            o8 = sb.tile([P, N], FP8, name="o8_%d" % m)
+            nc.vector.tensor_scalar(
+                out=o8[:, 0:V_CAST], in0=res[m][:, 0:V_CAST], scalar1=fac[:, 0:1], scalar2=None, op0=ALU.mult, saturate=False
+            )
+            nc.scalar.activation(
+                out=o8[:, V_CAST:N], in_=res[m][:, V_CAST:N], func=ACT.Identity, scale=fac[:, 0:1], bias=zero[:, 0:1], saturate=False
+            )
+            nc.sync.dma_start(out=o1v[:, m, :], in_=o8[:].bitcast(U8))

@@ -23,11 +23,14 @@ KP = P * PACK
 G = K // KP
 NH = 512
 J = N // NH
+CB = N // P
+CJ = NH // P
 EPS = 1e-5
 FLOPS = 2 * TOK * K * N
 
-V_SHARE = 256
+V_SHARE = 336
 V_CAST = 672
+V_NORM = 2
 
 
 def tile_dcadecoderblock_pb_kernel(tc, h_attn, x, attn_out_W, attn_out_b, attn_norm_g, attn_norm_b, out_0, out_1):
@@ -50,39 +53,43 @@ def tile_dcadecoderblock_pb_kernel(tc, h_attn, x, attn_out_W, attn_out_b, attn_n
         ident = sb.tile([P, P], F32, name="ident")
         masks.make_identity(nc, ident[:])
 
-        chunks = [(g, j) for g in range(G) for j in range(J)]
+        g16 = sb.tile([P, CB], BF16, name="g16")
+        be16 = sb.tile([P, CB], BF16, name="be16")
+        with nc.allow_non_contiguous_dma(reason="two small vectors, one element a partition"):
+            nc.scalar.dma_start(out=g16[:], in_=attn_norm_g.rearrange("(c p) -> p c", p=P))
+            nc.scalar.dma_start(out=be16[:], in_=attn_norm_b.rearrange("(c p) -> p c", p=P))
+        g_col = sb.tile([P, CB], F32, name="g_col")
+        nc.vector.tensor_copy(out=g_col[:], in_=g16[:])
+        be_col = sb.tile([P, CB], F32, name="be_col")
+        nc.vector.tensor_copy(out=be_col[:], in_=be16[:])
+
         w_raw = {}
         h_sb = {}
+        x_sb = {}
 
-        def load_w(c):
-            g, j = c
-            t = sb.tile([P, PACK, NH], BF16, name="wraw%d%d" % c)
+        def load_w(g, j):
+            t = sb.tile([P, PACK, NH], BF16, name="wraw%d%d" % (g, j))
             nc.sync.dma_start(
                 out=t[:],
                 in_=attn_out_W[g * KP : (g + 1) * KP, j * NH : (j + 1) * NH].rearrange("(p t) n -> p t n", t=PACK),
             )
-            w_raw[c] = t
+            w_raw[(g, j)] = t
 
         def load_h(m):
             t = sb.tile([P, K], BF16, name="hsb%d" % m)
             nc.sync.dma_start(out=t[:], in_=hv[:, m, :])
             h_sb[m] = t
 
-        load_w(chunks[0])
+        load_w(0, 0)
         load_h(0)
         load_h(1)
-        load_w(chunks[1])
+        load_w(1, 0)
         load_h(2)
         load_h(3)
-        load_w(chunks[2])
-        load_w(chunks[3])
         b_bc = sb.tile([P, N], BF16, name="b_bc")
         nc.sync.dma_start(out=b_bc[:], in_=attn_out_b.partition_broadcast(P))
-        g_bc = sb.tile([P, N], BF16, name="g_bc")
-        nc.sync.dma_start(out=g_bc[:], in_=attn_norm_g.partition_broadcast(P))
-        be_bc = sb.tile([P, N], BF16, name="be_bc")
-        nc.sync.dma_start(out=be_bc[:], in_=attn_norm_b.partition_broadcast(P))
-        x_sb = {}
+        load_w(0, 1)
+        load_w(1, 1)
         for m in range(MT):
             t = sb.tile([P, N], BF16, name="xsb%d" % m)
             nc.sync.dma_start(out=t[:], in_=xv[:, m, :])
@@ -96,20 +103,20 @@ def tile_dcadecoderblock_pb_kernel(tc, h_attn, x, attn_out_W, attn_out_b, attn_n
         h_scales = {}
         acc = {}
 
-        def interleave_w(c):
-            grp = sb.tile([P, NH * PACK], BF16, name="wgrp%d%d" % c, align_bytes=64)
+        def interleave_w(g, j):
+            grp = sb.tile([P, NH * PACK], BF16, name="wgrp%d%d" % (g, j), align_bytes=64)
             g3 = grp[:].rearrange("p (n t) -> p n t", t=PACK)
-            raw = w_raw[c]
+            raw = w_raw[(g, j)]
             nc.vector.tensor_copy(out=g3[:, 0:V_SHARE, :], in_=raw[:, :, 0:V_SHARE].rearrange("p t n -> p n t"))
             nc.scalar.copy(out=g3[:, V_SHARE:NH, :], in_=raw[:, :, V_SHARE:NH].rearrange("p t n -> p n t"))
-            w_grp[c] = grp
+            w_grp[(g, j)] = grp
 
-        def quantize_w(c):
-            codes = sb.tile([P, NH], U32, name="wc%d%d" % c, align_bytes=64)
-            scales = sb.tile([P, NH], U8, name="ws%d%d" % c, align_bytes=64)
-            nc.vector.quantize_mx(out=codes[:].bitcast(FP8X4), scales=scales[:], in_=w_grp[c][:])
-            w_codes[c] = codes
-            w_scales[c] = scales
+        def quantize_w(g, j):
+            codes = sb.tile([P, NH], U32, name="wc%d%d" % (g, j), align_bytes=64)
+            scales = sb.tile([P, NH], U8, name="ws%d%d" % (g, j), align_bytes=64)
+            nc.vector.quantize_mx(out=codes[:].bitcast(FP8X4), scales=scales[:], in_=w_grp[(g, j)][:])
+            w_codes[(g, j)] = codes
+            w_scales[(g, j)] = scales
 
         def transpose_h(m):
             words = h_sb[m][:].bitcast(F32)
@@ -131,104 +138,140 @@ def tile_dcadecoderblock_pb_kernel(tc, h_attn, x, attn_out_W, attn_out_b, attn_n
             h_codes[m] = codes
             h_scales[m] = scales
 
-        def mx(c, m):
-            g, j = c
+        def mx(g, j, m):
             if g == 0:
                 acc[(m, j)] = ps.tile([P, NH], F32, name="acc%d%d" % (m, j), tag="bank")
             nc.tensor.matmul_mx(
                 out=acc[(m, j)][:],
                 lhsT=h_codes[m][:, g * P : (g + 1) * P].bitcast(FP8X4),
                 lhsT_scale=h_scales[m][:, g * P : (g + 1) * P],
-                rhs=w_codes[c][:].bitcast(FP8X4),
-                rhs_scale=w_scales[c][:],
+                rhs=w_codes[(g, j)][:].bitcast(FP8X4),
+                rhs_scale=w_scales[(g, j)][:],
                 start=(g == 0),
                 stop=(g == G - 1),
             )
 
-        interleave_w(chunks[0])
+        interleave_w(0, 0)
         transpose_h(0)
         transpose_h(1)
-        interleave_w(chunks[1])
-        quantize_w(chunks[0])
+        interleave_w(1, 0)
+        quantize_w(0, 0)
         quantize_h(0)
         quantize_h(1)
         transpose_h(2)
         transpose_h(3)
-        mx(chunks[0], 0)
-        mx(chunks[0], 1)
-        interleave_w(chunks[2])
-        quantize_w(chunks[1])
+        mx(0, 0, 0)
+        mx(0, 0, 1)
+        quantize_w(1, 0)
         quantize_h(2)
         quantize_h(3)
-        mx(chunks[0], 2)
-        mx(chunks[0], 3)
+        mx(0, 0, 2)
+        mx(0, 0, 3)
         for m in range(MT):
-            mx(chunks[1], m)
-        interleave_w(chunks[3])
-        quantize_w(chunks[2])
+            mx(1, 0, m)
+        interleave_w(0, 1)
+        interleave_w(1, 1)
+        quantize_w(0, 1)
         for m in range(MT):
-            mx(chunks[2], m)
-        quantize_w(chunks[3])
+            mx(0, 1, m)
+        quantize_w(1, 1)
         for m in range(MT):
-            mx(chunks[3], m)
+            mx(1, 1, m)
 
-        am = sb.tile([P, MT], F32, name="am")
-        res = {}
+        o = {}
+        sums = {}
+        ssq = {}
+        negs = {}
+        junk = sb.tile([P, NH], BF16, name="junk")
+        res = sb.tile([P, MT, N + 8], F32, name="res")
+        nc.vector.memset(res[:, 0, N : N + 1], 0.0)
+
+        def bias_add(m, j):
+            cols = slice(j * NH, (j + 1) * NH)
+            nc.vector.scalar_tensor_tensor(
+                out=o[m][:, cols], in0=acc[(m, j)][:], scalar=1.0, in1=b_bc[:, cols],
+                op0=ALU.mult, op1=ALU.add, accum_out=sums[m][:, j : j + 1],
+            )
+
+        def squares(m, j):
+            cols = slice(j * NH, (j + 1) * NH)
+            nc.scalar.activation(
+                out=junk[:], in_=o[m][:, cols], func=ACT.Square, bias=negs[m][:, 0:1], scale=1.0, accum_out=ssq[m][:, j : j + 1]
+            )
+
         for m in range(MT):
-            o = sb.tile([P, N], F32, name="o%d" % m)
-            sums = sb.tile([P, J], F32, name="sums%d" % m)
-            for j in range(J):
-                nc.vector.scalar_tensor_tensor(
-                    out=o[:, j * NH : (j + 1) * NH],
-                    in0=acc[(m, j)][:],
-                    scalar=1.0,
-                    in1=b_bc[:, j * NH : (j + 1) * NH],
-                    op0=ALU.mult,
-                    op1=ALU.add,
-                    accum_out=sums[:, j : j + 1],
-                )
-            negmu = sb.tile([P, 1], F32, name="negmu%d" % m)
-            nc.vector.tensor_scalar(
-                out=negmu[:], in0=sums[:, 0:1], scalar1=sums[:, 1:2], scalar2=-1.0 / N, op0=ALU.add, op1=ALU.mult
-            )
-            junk = sb.tile([P, N], BF16, name="junk%d" % m)
-            ssq = sb.tile([P, 1], F32, name="ssq%d" % m)
-            nc.scalar.activation(out=junk[:], in_=o[:], func=ACT.Square, bias=negmu[:, 0:1], scale=1.0, accum_out=ssq[:])
-            std = sb.tile([P, 1], F32, name="std%d" % m)
-            nc.scalar.activation(out=std[:], in_=ssq[:], func=ACT.Sqrt, bias=EPS, scale=1.0 / N)
-            t = sb.tile([P, N], F32, name="t%d" % m)
-            nc.vector.scalar_tensor_tensor(
-                out=t[:], in0=o[:], scalar=negmu[:, 0:1], in1=g_bc[:], op0=ALU.add, op1=ALU.mult
-            )
-            xb = sb.tile([P, N], F32, name="xb%d" % m)
-            nc.vector.tensor_tensor(out=xb[:], in0=x_sb[m][:], in1=be_bc[:], op=ALU.add)
-            rstd = sb.tile([P, 1], F32, name="rstd%d" % m)
-            nc.vector.reciprocal(out=rstd[:], in_=std[:])
-            r = sb.tile([P, N], F32, name="res%d" % m)
-            nc.vector.scalar_tensor_tensor(
-                out=r[:], in0=t[:], scalar=rstd[:, 0:1], in1=xb[:], op0=ALU.mult, op1=ALU.add
-            )
-            nc.sync.dma_start(out=o0v[:, m, :], in_=r[:])
-            nc.vector.tensor_reduce(out=am[:, m : m + 1], in_=r[:], axis=AX.X, op=ALU.max, apply_absolute_value=True)
-            res[m] = r
+            o[m] = sb.tile([P, N], F32, name="o%d" % m)
+            sums[m] = sb.tile([P, J], F32, name="sums%d" % m)
+            ssq[m] = sb.tile([P, J], F32, name="ssq%d" % m)
+            negs[m] = sb.tile([P, 1], F32, name="negs%d" % m)
+            bias_add(m, 0)
+            nc.vector.tensor_scalar(out=negs[m][:], in0=sums[m][:, 0:1], scalar1=-1.0 / NH, scalar2=None, op0=ALU.mult)
+            squares(m, 0)
 
         pm = sb.tile([P, 1], F32, name="pm")
-        nc.vector.tensor_reduce(out=pm[:], in_=am[:], axis=AX.X, op=ALU.max)
+        for m in range(MT):
+            bias_add(m, 1)
+            squares(m, 1)
+            s0 = sums[m][:, 0:1]
+            s1 = sums[m][:, 1:2]
+            negmu = sb.tile([P, 1], F32, name="negmu%d" % m)
+            nc.vector.tensor_scalar(out=negmu[:], in0=s0, scalar1=s1, scalar2=-1.0 / N, op0=ALU.add, op1=ALU.mult)
+            d = sb.tile([P, 1], F32, name="d%d" % m)
+            nc.vector.tensor_scalar(out=d[:], in0=s1, scalar1=s0, scalar2=1.0 / N, op0=ALU.subtract, op1=ALU.mult)
+            w = sb.tile([P, 1], F32, name="w%d" % m)
+            nc.vector.tensor_scalar(out=w[:], in0=d[:], scalar1=d[:, 0:1], scalar2=EPS, op0=ALU.mult, op1=ALU.subtract)
+            vb = sb.tile([P, 1], F32, name="vb%d" % m)
+            nc.vector.tensor_scalar(out=vb[:], in0=ssq[m][:, 0:1], scalar1=1.0 / N, scalar2=w[:, 0:1], op0=ALU.mult, op1=ALU.subtract)
+            std = sb.tile([P, 1], F32, name="std%d" % m)
+            nc.scalar.activation(out=std[:], in_=ssq[m][:, 1:2], func=ACT.Sqrt, bias=vb[:, 0:1], scale=1.0 / N)
+            rstd = sb.tile([P, 1], F32, name="rstd%d" % m)
+            nc.vector.reciprocal(out=rstd[:], in_=std[:])
+            nrm = sb.tile([P, N], F32, name="nrm%d" % m)
+            yT = sb.tile([P, CB, P], F32, name="yT%d" % m)
+            eng = nc.vector if m < V_NORM else nc.gpsimd
+            for j in range(J):
+                cols = slice(j * NH, (j + 1) * NH)
+                eng.tensor_scalar(
+                    out=nrm[:, cols], in0=o[m][:, cols], scalar1=negmu[:, 0:1], scalar2=rstd[:, 0:1], op0=ALU.add, op1=ALU.mult
+                )
+            for j in range(J):
+                nT = ps.tile([P, CJ, P], F32, name="nT%d%d" % (m, j), tag="bank")
+                for i in range(CJ):
+                    c = j * CJ + i
+                    nc.tensor.transpose(nT[:, i, :], nrm[:, c * P : (c + 1) * P], ident[:])
+                for i in range(CJ):
+                    c = j * CJ + i
+                    nc.scalar.activation(
+                        out=yT[:, c, :], in_=nT[:, i, :], func=ACT.Identity, scale=g_col[:, c : c + 1], bias=be_col[:, c : c + 1]
+                    )
+            for j in range(J):
+                cols = slice(j * NH, (j + 1) * NH)
+                y = ps.tile([P, CJ, P], F32, name="y%d%d" % (m, j), tag="bank")
+                for i in range(CJ):
+                    nc.tensor.transpose(y[:, i, :], yT[:, j * CJ + i, :], ident[:])
+                nc.vector.tensor_tensor(
+                    out=res[:, m, cols], in0=y[:].rearrange("p i q -> p (i q)"), in1=x_sb[m][:, cols], op=ALU.add
+                )
+            nc.sync.dma_start(out=o0v[:, m, :], in_=res[:, m, 0:N])
+            nxt = res[:, m + 1, N : N + 1] if m + 1 < MT else pm[:]
+            nc.vector.tensor_reduce(out=nxt, in_=res[:, m, 0 : N + 1], axis=AX.X, op=ALU.max, apply_absolute_value=True)
+
+        rp = sb.tile([P, 1], F32, name="rp")
+        nc.vector.reciprocal(out=rp[:], in_=pm[:])
         bt = ps.tile([P, P], F32, name="bt", tag="bank")
-        nc.tensor.transpose(bt[:], pm[:, 0:1].to_broadcast([P, P]), ident[:])
-        gm = sb.tile([P, 1], F32, name="gm")
-        nc.vector.tensor_reduce(out=gm[:], in_=bt[:], axis=AX.X, op=ALU.max)
-        rg = sb.tile([P, 1], F32, name="rg")
-        nc.vector.reciprocal(out=rg[:], in_=gm[:])
+        nc.tensor.transpose(bt[:], rp[:, 0:1].to_broadcast([P, P]), ident[:])
+        scaled = sb.tile([P, P], F32, name="scaled")
         fac = sb.tile([P, 1], F32, name="fac")
-        nc.vector.tensor_scalar(out=fac[:], in0=rg[:], scalar1=448.0, scalar2=None, op0=ALU.mult)
+        nc.vector.tensor_scalar(
+            out=scaled[:], in0=bt[:], scalar1=448.0, scalar2=None, op0=ALU.mult, op1=ALU.min, accum_out=fac[:]
+        )
 
         for m in range(MT):
             o8 = sb.tile([P, N], FP8, name="o8_%d" % m)
             nc.vector.tensor_scalar(
-                out=o8[:, 0:V_CAST], in0=res[m][:, 0:V_CAST], scalar1=fac[:, 0:1], scalar2=None, op0=ALU.mult, saturate=False
+                out=o8[:, 0:V_CAST], in0=res[:, m, 0:V_CAST], scalar1=fac[:, 0:1], scalar2=None, op0=ALU.mult, saturate=False
             )
             nc.scalar.activation(
-                out=o8[:, V_CAST:N], in_=res[m][:, V_CAST:N], func=ACT.Identity, scale=fac[:, 0:1], bias=zero[:, 0:1], saturate=False
+                out=o8[:, V_CAST:N], in_=res[:, m, V_CAST:N], func=ACT.Identity, scale=fac[:, 0:1], bias=zero[:, 0:1], saturate=False
             )
             nc.sync.dma_start(out=o1v[:, m, :], in_=o8[:].bitcast(U8))

@@ -49,19 +49,21 @@ def tile_dcadecoderblock_pb_kernel(tc, h_attn, x, attn_out_W, attn_out_b, attn_n
         zero = sb.tile([P, 1], F32, name="zero")
         nc.vector.memset(zero[:], 0.0)
         warm = sb.tile([P, 1], F32, name="warm")
-        nc.scalar.activation(out=warm[:], in_=one[:], func=ACT.Sqrt)
         ident = sb.tile([P, P], F32, name="ident")
         masks.make_identity(nc, ident[:])
 
-        g16 = sb.tile([P, CB], BF16, name="g16")
-        be16 = sb.tile([P, CB], BF16, name="be16")
-        with nc.allow_non_contiguous_dma(reason="two small vectors, one element a partition"):
-            nc.scalar.dma_start(out=g16[:], in_=attn_norm_g.rearrange("(c p) -> p c", p=P))
-            nc.scalar.dma_start(out=be16[:], in_=attn_norm_b.rearrange("(c p) -> p c", p=P))
-        g_col = sb.tile([P, CB], F32, name="g_col")
-        nc.vector.tensor_copy(out=g_col[:], in_=g16[:])
-        be_col = sb.tile([P, CB], F32, name="be_col")
-        nc.vector.tensor_copy(out=be_col[:], in_=be16[:])
+        ones16 = sb.tile([P, P], BF16, name="ones16")
+        nc.vector.memset(ones16[:], 1.0)
+        brow = sb.tile([P, N], BF16, name="brow")
+        nc.vector.memset(brow[:].bitcast(F32), 0.0)
+        grow = sb.tile([P, P], BF16, name="grow")
+        nc.vector.memset(grow[:].bitcast(F32), 0.0)
+        nc.scalar.dma_start(out=brow[0:1, :], in_=attn_out_b.rearrange("(o n) -> o n", o=1))
+        nc.scalar.dma_start(out=grow[0:CB, :], in_=attn_norm_g.rearrange("(c p) -> c p", p=P))
+        nc.scalar.dma_start(out=grow[CB : 2 * CB, :], in_=attn_norm_b.rearrange("(c p) -> c p", p=P))
+        nc.scalar.activation(out=warm[:], in_=one[:], func=ACT.Sqrt)
+        ident16 = sb.tile([P, P], BF16, name="ident16")
+        nc.vector.tensor_copy(out=ident16[:], in_=ident[:])
 
         w_raw = {}
         h_sb = {}
@@ -86,14 +88,22 @@ def tile_dcadecoderblock_pb_kernel(tc, h_attn, x, attn_out_W, attn_out_b, attn_n
         load_w(1, 0)
         load_h(2)
         load_h(3)
-        b_bc = sb.tile([P, N], BF16, name="b_bc")
-        nc.sync.dma_start(out=b_bc[:], in_=attn_out_b.partition_broadcast(P))
         load_w(0, 1)
         load_w(1, 1)
         for m in range(MT):
             t = sb.tile([P, N], BF16, name="xsb%d" % m)
             nc.sync.dma_start(out=t[:], in_=xv[:, m, :])
             x_sb[m] = t
+
+        b_bc = sb.tile([P, N], F32, name="b_bc")
+        for j in range(J):
+            bb = ps.tile([P, NH], F32, name="bb%d" % j, tag="bank")
+            nc.tensor.matmul(out=bb[:], lhsT=ones16[:], rhs=brow[:, j * NH : (j + 1) * NH], start=True, stop=True)
+            nc.scalar.copy(out=b_bc[:, j * NH : (j + 1) * NH], in_=bb[:])
+        gbp = ps.tile([P, 2 * CB], F32, name="gbp", tag="bank")
+        nc.tensor.matmul(out=gbp[:], lhsT=grow[:], rhs=ident16[:, 0 : 2 * CB], start=True, stop=True)
+        gb = sb.tile([P, 2 * CB], F32, name="gb")
+        nc.vector.tensor_copy(out=gb[:], in_=gbp[:])
 
         w_grp = {}
         w_codes = {}
@@ -242,7 +252,7 @@ def tile_dcadecoderblock_pb_kernel(tc, h_attn, x, attn_out_W, attn_out_b, attn_n
                 for i in range(CJ):
                     c = j * CJ + i
                     nc.scalar.activation(
-                        out=yT[:, c, :], in_=nT[:, i, :], func=ACT.Identity, scale=g_col[:, c : c + 1], bias=be_col[:, c : c + 1]
+                        out=yT[:, c, :], in_=nT[:, i, :], func=ACT.Identity, scale=gb[:, c : c + 1], bias=gb[:, CB + c : CB + c + 1]
                     )
             for j in range(J):
                 cols = slice(j * NH, (j + 1) * NH)

@@ -52,16 +52,9 @@ def tile_dcadecoderblock_pb_kernel(tc, h_attn, x, attn_out_W, attn_out_b, attn_n
         ident = sb.tile([P, P], F32, name="ident")
         masks.make_identity(nc, ident[:])
 
-        ones16 = sb.tile([P, P], BF16, name="ones16")
-        nc.vector.memset(ones16[:], 1.0)
-        brow = sb.tile([P, N], BF16, name="brow")
-        nc.vector.memset(brow[:].bitcast(F32), 0.0)
-        grow = sb.tile([P, P], BF16, name="grow")
-        nc.vector.memset(grow[:].bitcast(F32), 0.0)
-        nc.scalar.dma_start(out=brow[0:1, :], in_=attn_out_b.rearrange("(o n) -> o n", o=1))
-        nc.scalar.dma_start(out=grow[0:CB, :], in_=attn_norm_g.rearrange("(c p) -> c p", p=P))
-        nc.scalar.dma_start(out=grow[CB : 2 * CB, :], in_=attn_norm_b.rearrange("(c p) -> c p", p=P))
         nc.scalar.activation(out=warm[:], in_=one[:], func=ACT.Sqrt)
+        rows = sb.tile([P, P], BF16, name="rows")
+        nc.vector.memset(rows[:].bitcast(F32), 0.0)
         ident16 = sb.tile([P, P], BF16, name="ident16")
         nc.vector.tensor_copy(out=ident16[:], in_=ident[:])
 
@@ -85,6 +78,8 @@ def tile_dcadecoderblock_pb_kernel(tc, h_attn, x, attn_out_W, attn_out_b, attn_n
         load_w(0, 0)
         load_h(0)
         load_h(1)
+        for i, vec in enumerate((attn_norm_g, attn_norm_b, attn_out_b)):
+            nc.sync.dma_start(out=rows[i * CB : (i + 1) * CB, :], in_=vec.rearrange("(c p) -> c p", p=P))
         load_w(1, 0)
         load_h(2)
         load_h(3)
@@ -96,14 +91,18 @@ def tile_dcadecoderblock_pb_kernel(tc, h_attn, x, attn_out_W, attn_out_b, attn_n
             x_sb[m] = t
 
         b_bc = sb.tile([P, N], F32, name="b_bc")
-        for j in range(J):
-            bb = ps.tile([P, NH], F32, name="bb%d" % j, tag="bank")
-            nc.tensor.matmul(out=bb[:], lhsT=ones16[:], rhs=brow[:, j * NH : (j + 1) * NH], start=True, stop=True)
-            nc.scalar.copy(out=b_bc[:, j * NH : (j + 1) * NH], in_=bb[:])
-        gbp = ps.tile([P, 2 * CB], F32, name="gbp", tag="bank")
-        nc.tensor.matmul(out=gbp[:], lhsT=grow[:], rhs=ident16[:, 0 : 2 * CB], start=True, stop=True)
         gb = sb.tile([P, 2 * CB], F32, name="gb")
-        nc.vector.tensor_copy(out=gb[:], in_=gbp[:])
+
+        def lay_out_vectors():
+            gbp = ps.tile([P, 2 * CB], F32, name="gbp", tag="bank")
+            nc.tensor.matmul(out=gbp[:], lhsT=rows[:], rhs=ident16[:, 0 : 2 * CB], start=True, stop=True)
+            nc.vector.tensor_copy(out=gb[:], in_=gbp[:])
+            for j in range(J):
+                bb = ps.tile([P, CJ, P], F32, name="bb%d" % j, tag="bank")
+                for i in range(CJ):
+                    r = 2 * CB + j * CJ + i
+                    nc.tensor.matmul(out=bb[:, i, :], lhsT=ident16[:, r : r + 1].to_broadcast([P, P]), rhs=rows[:], start=True, stop=True)
+                nc.scalar.copy(out=b_bc[:, j * NH : (j + 1) * NH], in_=bb[:].rearrange("p i q -> p (i q)"))
 
         w_grp = {}
         w_codes = {}
@@ -117,8 +116,14 @@ def tile_dcadecoderblock_pb_kernel(tc, h_attn, x, attn_out_W, attn_out_b, attn_n
             grp = sb.tile([P, NH * PACK], BF16, name="wgrp%d%d" % (g, j), align_bytes=64)
             g3 = grp[:].rearrange("p (n t) -> p n t", t=PACK)
             raw = w_raw[(g, j)]
-            nc.vector.tensor_copy(out=g3[:, 0:V_SHARE, :], in_=raw[:, :, 0:V_SHARE].rearrange("p t n -> p n t"))
-            nc.scalar.copy(out=g3[:, V_SHARE:NH, :], in_=raw[:, :, V_SHARE:NH].rearrange("p t n -> p n t"))
+            nc.vector.tensor_copy(
+                out=g3[:, 0:V_SHARE, :].rearrange("p (c i) t -> p c t i", i=4),
+                in_=raw[:, :, 0:V_SHARE].rearrange("p t (c i) -> p c t i", i=4),
+            )
+            nc.scalar.copy(
+                out=g3[:, V_SHARE:NH, :].rearrange("p (c i) t -> p c t i", i=4),
+                in_=raw[:, :, V_SHARE:NH].rearrange("p t (c i) -> p c t i", i=4),
+            )
             w_grp[(g, j)] = grp
 
         def quantize_w(g, j):
@@ -164,6 +169,7 @@ def tile_dcadecoderblock_pb_kernel(tc, h_attn, x, attn_out_W, attn_out_b, attn_n
         interleave_w(0, 0)
         transpose_h(0)
         transpose_h(1)
+        lay_out_vectors()
         interleave_w(1, 0)
         quantize_w(0, 0)
         quantize_h(0)

@@ -14,31 +14,33 @@ ACT = mybir.ActivationFunctionType
 AX = mybir.AxisListType
 
 P = 128
-TOK = 512
+TOKENS = 512
 K = 1024
 N = 1024
-MT = TOK // P
+TILES = TOKENS // P
 PACK = 4
-KP = P * PACK
-G = K // KP
-NH = 512
-J = N // NH
-CB = N // P
-CJ = NH // P
+K_PASS = P * PACK
+PASSES = K // K_PASS
+HALF = 512
+HALVES = N // HALF
+BLOCKS = N // P
+BLOCKS_PER_HALF = HALF // P
 EPS = 1e-5
-FLOPS = 2 * TOK * K * N
+FP8_MAX = 448.0
+PAD = 8
+FLOPS = 2 * TOKENS * K * N
 
-V_SHARE = 336
+V_INTERLEAVE = 336
 V_CAST = 672
-V_NORM = 2
+V_NORMALISE = 2
 
 
 def tile_dcadecoderblock_pb_kernel(tc, h_attn, x, attn_out_W, attn_out_b, attn_norm_g, attn_norm_b, out_0, out_1):
     nc = tc.nc
-    hv = h_attn.flatten_outer_dims().rearrange("(p m) k -> p m k", m=MT)
-    xv = x.flatten_outer_dims().rearrange("(p m) n -> p m n", m=MT)
-    o0v = out_0.flatten_outer_dims().rearrange("(p m) n -> p m n", m=MT)
-    o1v = out_1.flatten_outer_dims().rearrange("(p m) n -> p m n", m=MT)
+    h_view = h_attn.flatten_outer_dims().rearrange("(p m) k -> p m k", m=TILES)
+    x_view = x.flatten_outer_dims().rearrange("(p m) n -> p m n", m=TILES)
+    out0_view = out_0.flatten_outer_dims().rearrange("(p m) n -> p m n", m=TILES)
+    out1_view = out_1.flatten_outer_dims().rearrange("(p m) n -> p m n", m=TILES)
 
     with ExitStack() as ctx:
         sb = ctx.enter_context(tc.tile_pool(name="sb", bufs=1))
@@ -48,13 +50,12 @@ def tile_dcadecoderblock_pb_kernel(tc, h_attn, x, attn_out_W, attn_out_b, attn_n
         nc.vector.memset(one[:], 1.0)
         zero = sb.tile([P, 1], F32, name="zero")
         nc.vector.memset(zero[:], 0.0)
-        warm = sb.tile([P, 1], F32, name="warm")
-        ident = sb.tile([P, P], F32, name="ident")
-        masks.make_identity(nc, ident[:])
-
-        nc.scalar.activation(out=warm[:], in_=one[:], func=ACT.Sqrt)
         rows = sb.tile([P, P], BF16, name="rows")
         nc.vector.memset(rows[:].bitcast(F32), 0.0)
+        warm = sb.tile([P, 1], F32, name="warm")
+        nc.scalar.activation(out=warm[:], in_=one[:], func=ACT.Abs_reciprocal_sqrt)
+        ident = sb.tile([P, P], F32, name="ident")
+        masks.make_identity(nc, ident[:])
         ident16 = sb.tile([P, P], BF16, name="ident16")
         nc.vector.tensor_copy(out=ident16[:], in_=ident[:])
 
@@ -63,99 +64,105 @@ def tile_dcadecoderblock_pb_kernel(tc, h_attn, x, attn_out_W, attn_out_b, attn_n
         x_sb = {}
 
         def load_w(g, j):
-            t = sb.tile([P, PACK, NH], BF16, name="wraw%d%d" % (g, j))
+            t = sb.tile([P, PACK, HALF], BF16, name="wraw%d%d" % (g, j))
             nc.sync.dma_start(
                 out=t[:],
-                in_=attn_out_W[g * KP : (g + 1) * KP, j * NH : (j + 1) * NH].rearrange("(p t) n -> p t n", t=PACK),
+                in_=attn_out_W[g * K_PASS : (g + 1) * K_PASS, j * HALF : (j + 1) * HALF].rearrange("(p t) n -> p t n", t=PACK),
             )
             w_raw[(g, j)] = t
 
         def load_h(m):
             t = sb.tile([P, K], BF16, name="hsb%d" % m)
-            nc.sync.dma_start(out=t[:], in_=hv[:, m, :])
+            nc.sync.dma_start(out=t[:], in_=h_view[:, m, :])
             h_sb[m] = t
+
+        def load_x(m):
+            t = sb.tile([P, N], BF16, name="xsb%d" % m)
+            nc.sync.dma_start(out=t[:], in_=x_view[:, m, :])
+            x_sb[m] = t
 
         load_w(0, 0)
         load_h(0)
         load_h(1)
         for i, vec in enumerate((attn_norm_g, attn_norm_b, attn_out_b)):
-            nc.sync.dma_start(out=rows[i * CB : (i + 1) * CB, :], in_=vec.rearrange("(c p) -> c p", p=P))
+            nc.sync.dma_start(out=rows[i * BLOCKS : (i + 1) * BLOCKS, :], in_=vec.rearrange("(c p) -> c p", p=P))
         load_w(1, 0)
-        load_h(2)
-        load_h(3)
         load_w(0, 1)
         load_w(1, 1)
-        for m in range(MT):
-            t = sb.tile([P, N], BF16, name="xsb%d" % m)
-            nc.sync.dma_start(out=t[:], in_=xv[:, m, :])
-            x_sb[m] = t
+        load_h(2)
+        load_h(3)
+        for m in range(TILES):
+            load_x(m)
 
-        b_bc = sb.tile([P, N], F32, name="b_bc")
-        gb = sb.tile([P, 2 * CB], F32, name="gb")
+        b_all = sb.tile([P, N], BF16, name="b_bc")
+        gain_shift_cols = sb.tile([P, 2 * BLOCKS], F32, name="gb")
 
         def lay_out_vectors():
-            gbp = ps.tile([P, 2 * CB], F32, name="gbp", tag="bank")
-            nc.tensor.matmul(out=gbp[:], lhsT=rows[:], rhs=ident16[:, 0 : 2 * CB], start=True, stop=True)
-            nc.vector.tensor_copy(out=gb[:], in_=gbp[:])
-            for j in range(J):
-                bb = ps.tile([P, CJ, P], F32, name="bb%d" % j, tag="bank")
-                for i in range(CJ):
-                    r = 2 * CB + j * CJ + i
-                    nc.tensor.matmul(out=bb[:, i, :], lhsT=ident16[:, r : r + 1].to_broadcast([P, P]), rhs=rows[:], start=True, stop=True)
-                nc.scalar.copy(out=b_bc[:, j * NH : (j + 1) * NH], in_=bb[:].rearrange("p i q -> p (i q)"))
+            cols_ps = ps.tile([P, 2 * BLOCKS], F32, name="gbp", tag="bank")
+            nc.tensor.matmul(out=cols_ps[:], lhsT=rows[:], rhs=ident16[:, 0 : 2 * BLOCKS], start=True, stop=True)
+            nc.vector.tensor_copy(out=gain_shift_cols[:], in_=cols_ps[:])
+            b_ps = ps.tile([P, BLOCKS, P], BF16, name="bb", tag="bank")
+            for c in range(BLOCKS):
+                r = 2 * BLOCKS + c
+                nc.tensor.matmul(out=b_ps[:, c, :], lhsT=ident16[:, r : r + 1].to_broadcast([P, P]), rhs=rows[:], start=True, stop=True)
+            nc.scalar.copy(out=b_all[:], in_=b_ps[:].rearrange("p c q -> p (c q)"))
 
-        w_grp = {}
+        w_grouped = {}
         w_codes = {}
         w_scales = {}
-        h_grp = {}
+        h_turned = {}
+        h_grouped = {}
         h_codes = {}
         h_scales = {}
         acc = {}
 
         def interleave_w(g, j):
-            grp = sb.tile([P, NH * PACK], BF16, name="wgrp%d%d" % (g, j), align_bytes=64)
-            g3 = grp[:].rearrange("p (n t) -> p n t", t=PACK)
+            grouped = sb.tile([P, HALF * PACK], BF16, name="wgrp%d%d" % (g, j), align_bytes=64)
+            dst = grouped[:].rearrange("p (n t) -> p n t", t=PACK)
             raw = w_raw[(g, j)]
             nc.vector.tensor_copy(
-                out=g3[:, 0:V_SHARE, :].rearrange("p (c i) t -> p c t i", i=4),
-                in_=raw[:, :, 0:V_SHARE].rearrange("p t (c i) -> p c t i", i=4),
+                out=dst[:, 0:V_INTERLEAVE, :].rearrange("p (c i) t -> p c t i", i=4),
+                in_=raw[:, :, 0:V_INTERLEAVE].rearrange("p t (c i) -> p c t i", i=4),
             )
             nc.scalar.copy(
-                out=g3[:, V_SHARE:NH, :].rearrange("p (c i) t -> p c t i", i=4),
-                in_=raw[:, :, V_SHARE:NH].rearrange("p t (c i) -> p c t i", i=4),
+                out=dst[:, V_INTERLEAVE:HALF, :].rearrange("p (c i) t -> p c t i", i=4),
+                in_=raw[:, :, V_INTERLEAVE:HALF].rearrange("p t (c i) -> p c t i", i=4),
             )
-            w_grp[(g, j)] = grp
+            w_grouped[(g, j)] = grouped
 
         def quantize_w(g, j):
-            codes = sb.tile([P, NH], U32, name="wc%d%d" % (g, j), align_bytes=64)
-            scales = sb.tile([P, NH], U8, name="ws%d%d" % (g, j), align_bytes=64)
-            nc.vector.quantize_mx(out=codes[:].bitcast(FP8X4), scales=scales[:], in_=w_grp[(g, j)][:])
+            codes = sb.tile([P, HALF], U32, name="wc%d%d" % (g, j), align_bytes=64)
+            scales = sb.tile([P, HALF], U8, name="ws%d%d" % (g, j), align_bytes=64)
+            nc.vector.quantize_mx(out=codes[:].bitcast(FP8X4), scales=scales[:], in_=w_grouped[(g, j)][:])
             w_codes[(g, j)] = codes
             w_scales[(g, j)] = scales
 
-        def transpose_h(m):
+        def turn_h(m):
             words = h_sb[m][:].bitcast(F32)
-            xt = ps.tile([P, G, 2, P], F32, name="xt%d" % m, tag="bank")
-            for g in range(G):
+            turned = ps.tile([P, PASSES, 2, P], F32, name="xt%d" % m, tag="bank")
+            for g in range(PASSES):
                 for u in range(2):
-                    nc.tensor.transpose(xt[:, g, u, :], words[:, 256 * g + u : 256 * (g + 1) : 2], ident[:])
-            grp = sb.tile([P, G * P * PACK], BF16, name="hgrp%d" % m, align_bytes=64)
+                    nc.tensor.transpose(turned[:, g, u, :], words[:, 256 * g + u : 256 * (g + 1) : 2], ident[:])
+            h_turned[m] = turned
+
+        def copy_h(m):
+            grouped = sb.tile([P, PASSES * P * PACK], BF16, name="hgrp%d" % m, align_bytes=64)
             nc.scalar.copy(
-                out=grp[:].bitcast(F32).rearrange("p (g r u) -> p g r u", g=G, u=2),
-                in_=xt[:].rearrange("p g u r -> p g r u"),
+                out=grouped[:].bitcast(F32).rearrange("p (g r u) -> p g r u", g=PASSES, u=2),
+                in_=h_turned[m][:].rearrange("p g u r -> p g r u"),
             )
-            h_grp[m] = grp
+            h_grouped[m] = grouped
 
         def quantize_h(m):
-            codes = sb.tile([P, G * P], U32, name="hc%d" % m, align_bytes=64)
-            scales = sb.tile([P, G * P], U8, name="hs%d" % m, align_bytes=64)
-            nc.vector.quantize_mx(out=codes[:].bitcast(FP8X4), scales=scales[:], in_=h_grp[m][:])
+            codes = sb.tile([P, PASSES * P], U32, name="hc%d" % m, align_bytes=64)
+            scales = sb.tile([P, PASSES * P], U8, name="hs%d" % m, align_bytes=64)
+            nc.vector.quantize_mx(out=codes[:].bitcast(FP8X4), scales=scales[:], in_=h_grouped[m][:])
             h_codes[m] = codes
             h_scales[m] = scales
 
         def mx(g, j, m):
             if g == 0:
-                acc[(m, j)] = ps.tile([P, NH], F32, name="acc%d%d" % (m, j), tag="bank")
+                acc[(m, j)] = ps.tile([P, HALF], F32, name="acc%d%d" % (m, j), tag="bank")
             nc.tensor.matmul_mx(
                 out=acc[(m, j)][:],
                 lhsT=h_codes[m][:, g * P : (g + 1) * P].bitcast(FP8X4),
@@ -163,131 +170,143 @@ def tile_dcadecoderblock_pb_kernel(tc, h_attn, x, attn_out_W, attn_out_b, attn_n
                 rhs=w_codes[(g, j)][:].bitcast(FP8X4),
                 rhs_scale=w_scales[(g, j)][:],
                 start=(g == 0),
-                stop=(g == G - 1),
+                stop=(g == PASSES - 1),
             )
 
         interleave_w(0, 0)
-        transpose_h(0)
-        transpose_h(1)
+        for m in (0, 1):
+            turn_h(m)
+            copy_h(m)
         lay_out_vectors()
         interleave_w(1, 0)
         quantize_w(0, 0)
-        quantize_h(0)
-        quantize_h(1)
-        transpose_h(2)
-        transpose_h(3)
-        mx(0, 0, 0)
-        mx(0, 0, 1)
+        for m in (0, 1):
+            quantize_h(m)
+        for m in (0, 1):
+            mx(0, 0, m)
         quantize_w(1, 0)
-        quantize_h(2)
-        quantize_h(3)
-        mx(0, 0, 2)
-        mx(0, 0, 3)
-        for m in range(MT):
+        for m in (0, 1):
             mx(1, 0, m)
         interleave_w(0, 1)
         interleave_w(1, 1)
-        quantize_w(0, 1)
-        for m in range(MT):
-            mx(0, 1, m)
-        quantize_w(1, 1)
-        for m in range(MT):
-            mx(1, 1, m)
+        for g in range(PASSES):
+            quantize_w(g, 1)
+            for m in (0, 1):
+                mx(g, 1, m)
+        for m in (2, 3):
+            turn_h(m)
+        for m in (2, 3):
+            copy_h(m)
+        for m in (2, 3):
+            quantize_h(m)
+        for m in (2, 3):
+            for j in range(HALVES):
+                for g in range(PASSES):
+                    mx(g, j, m)
 
-        o = {}
-        sums = {}
-        ssq = {}
-        negs = {}
-        junk = sb.tile([P, NH], BF16, name="junk")
-        res = sb.tile([P, MT, N + 8], F32, name="res")
-        nc.vector.memset(res[:, 0, N : N + 1], 0.0)
+        squares_out = sb.tile([P, HALF], BF16, name="junk")
+        res_padded = sb.tile([P, TILES, PAD + N + PAD], F32, name="res")
+        res = res_padded[:, :, PAD : PAD + N]
+        amax_part = sb.tile([P, 1], F32, name="pm")
+        nc.vector.memset(res_padded[:, 0, PAD - 1 : PAD], 0.0)
 
-        def bias_add(m, j):
-            cols = slice(j * NH, (j + 1) * NH)
-            nc.vector.scalar_tensor_tensor(
-                out=o[m][:, cols], in0=acc[(m, j)][:], scalar=1.0, in1=b_bc[:, cols],
-                op0=ALU.mult, op1=ALU.add, accum_out=sums[m][:, j : j + 1],
-            )
+        for m in range(TILES):
+            o = sb.tile([P, N], F32, name="o%d" % m)
+            sums = sb.tile([P, HALVES], F32, name="sums%d" % m)
+            ssq = sb.tile([P, HALVES], F32, name="ssq%d" % m)
+            neg_shift = sb.tile([P, 1], F32, name="negs%d" % m)
 
-        def squares(m, j):
-            cols = slice(j * NH, (j + 1) * NH)
-            nc.scalar.activation(
-                out=junk[:], in_=o[m][:, cols], func=ACT.Square, bias=negs[m][:, 0:1], scale=1.0, accum_out=ssq[m][:, j : j + 1]
-            )
+            def bias_add(j):
+                cols = slice(j * HALF, (j + 1) * HALF)
+                nc.vector.scalar_tensor_tensor(
+                    out=o[:, cols], in0=acc[(m, j)][:], scalar=1.0, in1=b_all[:, cols],
+                    op0=ALU.mult, op1=ALU.add, accum_out=sums[:, j : j + 1],
+                )
 
-        for m in range(MT):
-            o[m] = sb.tile([P, N], F32, name="o%d" % m)
-            sums[m] = sb.tile([P, J], F32, name="sums%d" % m)
-            ssq[m] = sb.tile([P, J], F32, name="ssq%d" % m)
-            negs[m] = sb.tile([P, 1], F32, name="negs%d" % m)
-            bias_add(m, 0)
-            nc.vector.tensor_scalar(out=negs[m][:], in0=sums[m][:, 0:1], scalar1=-1.0 / NH, scalar2=None, op0=ALU.mult)
-            squares(m, 0)
+            def squares(j):
+                cols = slice(j * HALF, (j + 1) * HALF)
+                nc.scalar.activation(
+                    out=squares_out[:], in_=o[:, cols], func=ACT.Square, bias=neg_shift[:, 0:1], scale=1.0, accum_out=ssq[:, j : j + 1]
+                )
 
-        pm = sb.tile([P, 1], F32, name="pm")
-        for m in range(MT):
-            bias_add(m, 1)
-            squares(m, 1)
-            s0 = sums[m][:, 0:1]
-            s1 = sums[m][:, 1:2]
-            negmu = sb.tile([P, 1], F32, name="negmu%d" % m)
-            nc.vector.tensor_scalar(out=negmu[:], in0=s0, scalar1=s1, scalar2=-1.0 / N, op0=ALU.add, op1=ALU.mult)
+            bias_add(0)
+            nc.vector.tensor_scalar(out=neg_shift[:], in0=sums[:, 0:1], scalar1=-1.0 / HALF, scalar2=None, op0=ALU.mult)
+            squares(0)
+            bias_add(1)
+            squares(1)
+            s0 = sums[:, 0:1]
+            s1 = sums[:, 1:2]
+            neg_mean = sb.tile([P, 1], F32, name="negmu%d" % m)
             d = sb.tile([P, 1], F32, name="d%d" % m)
             nc.vector.tensor_scalar(out=d[:], in0=s1, scalar1=s0, scalar2=1.0 / N, op0=ALU.subtract, op1=ALU.mult)
+            nc.vector.tensor_scalar(out=neg_mean[:], in0=s0, scalar1=s1, scalar2=-1.0 / N, op0=ALU.add, op1=ALU.mult)
             w = sb.tile([P, 1], F32, name="w%d" % m)
             nc.vector.tensor_scalar(out=w[:], in0=d[:], scalar1=d[:, 0:1], scalar2=EPS, op0=ALU.mult, op1=ALU.subtract)
-            vb = sb.tile([P, 1], F32, name="vb%d" % m)
-            nc.vector.tensor_scalar(out=vb[:], in0=ssq[m][:, 0:1], scalar1=1.0 / N, scalar2=w[:, 0:1], op0=ALU.mult, op1=ALU.subtract)
-            std = sb.tile([P, 1], F32, name="std%d" % m)
-            nc.scalar.activation(out=std[:], in_=ssq[m][:, 1:2], func=ACT.Sqrt, bias=vb[:, 0:1], scale=1.0 / N)
+            rest = sb.tile([P, 1], F32, name="vb%d" % m)
+            nc.vector.tensor_scalar(out=rest[:], in0=ssq[:, 0:1], scalar1=1.0 / N, scalar2=w[:, 0:1], op0=ALU.mult, op1=ALU.subtract)
             rstd = sb.tile([P, 1], F32, name="rstd%d" % m)
-            nc.vector.reciprocal(out=rstd[:], in_=std[:])
-            nrm = sb.tile([P, N], F32, name="nrm%d" % m)
-            yT = sb.tile([P, CB, P], F32, name="yT%d" % m)
-            eng = nc.vector if m < V_NORM else nc.gpsimd
-            for j in range(J):
-                cols = slice(j * NH, (j + 1) * NH)
-                eng.tensor_scalar(
-                    out=nrm[:, cols], in0=o[m][:, cols], scalar1=negmu[:, 0:1], scalar2=rstd[:, 0:1], op0=ALU.add, op1=ALU.mult
-                )
-            for j in range(J):
-                nT = ps.tile([P, CJ, P], F32, name="nT%d%d" % (m, j), tag="bank")
-                for i in range(CJ):
-                    c = j * CJ + i
-                    nc.tensor.transpose(nT[:, i, :], nrm[:, c * P : (c + 1) * P], ident[:])
-                for i in range(CJ):
-                    c = j * CJ + i
-                    nc.scalar.activation(
-                        out=yT[:, c, :], in_=nT[:, i, :], func=ACT.Identity, scale=gb[:, c : c + 1], bias=gb[:, CB + c : CB + c + 1]
-                    )
-            for j in range(J):
-                cols = slice(j * NH, (j + 1) * NH)
-                y = ps.tile([P, CJ, P], F32, name="y%d%d" % (m, j), tag="bank")
-                for i in range(CJ):
-                    nc.tensor.transpose(y[:, i, :], yT[:, j * CJ + i, :], ident[:])
-                nc.vector.tensor_tensor(
-                    out=res[:, m, cols], in0=y[:].rearrange("p i q -> p (i q)"), in1=x_sb[m][:, cols], op=ALU.add
-                )
-            nc.sync.dma_start(out=o0v[:, m, :], in_=res[:, m, 0:N])
-            nxt = res[:, m + 1, N : N + 1] if m + 1 < MT else pm[:]
-            nc.vector.tensor_reduce(out=nxt, in_=res[:, m, 0 : N + 1], axis=AX.X, op=ALU.max, apply_absolute_value=True)
+            nc.scalar.activation(out=rstd[:], in_=ssq[:, 1:2], func=ACT.Abs_reciprocal_sqrt, bias=rest[:, 0:1], scale=1.0 / N)
 
-        rp = sb.tile([P, 1], F32, name="rp")
-        nc.vector.reciprocal(out=rp[:], in_=pm[:])
-        bt = ps.tile([P, P], F32, name="bt", tag="bank")
-        nc.tensor.transpose(bt[:], rp[:, 0:1].to_broadcast([P, P]), ident[:])
-        scaled = sb.tile([P, P], F32, name="scaled")
-        fac = sb.tile([P, 1], F32, name="fac")
+            normed = sb.tile([P, N], F32, name="nrm%d" % m)
+            scaled_t = sb.tile([P, BLOCKS, P], F32, name="yT%d" % m)
+            engine = nc.vector if m < V_NORMALISE else nc.gpsimd
+            for j in range(HALVES):
+                cols = slice(j * HALF, (j + 1) * HALF)
+                engine.tensor_scalar(
+                    out=normed[:, cols], in0=o[:, cols], scalar1=neg_mean[:, 0:1], scalar2=rstd[:, 0:1], op0=ALU.add, op1=ALU.mult
+                )
+            for j in range(HALVES):
+                normed_t = ps.tile([P, BLOCKS_PER_HALF, P], F32, name="nT%d%d" % (m, j), tag="bank")
+                for i in range(BLOCKS_PER_HALF):
+                    c = j * BLOCKS_PER_HALF + i
+                    nc.tensor.transpose(normed_t[:, i, :], normed[:, c * P : (c + 1) * P], ident[:])
+                for i in range(BLOCKS_PER_HALF):
+                    c = j * BLOCKS_PER_HALF + i
+                    nc.scalar.activation(
+                        out=scaled_t[:, c, :], in_=normed_t[:, i, :], func=ACT.Identity,
+                        scale=gain_shift_cols[:, c : c + 1], bias=gain_shift_cols[:, BLOCKS + c : BLOCKS + c + 1],
+                    )
+            last = m == TILES - 1
+            for j in range(HALVES):
+                cols = slice(j * HALF, (j + 1) * HALF)
+                scaled = ps.tile([P, BLOCKS_PER_HALF, P], F32, name="y%d%d" % (m, j), tag="bank")
+                for i in range(BLOCKS_PER_HALF):
+                    nc.tensor.transpose(scaled[:, i, :], scaled_t[:, j * BLOCKS_PER_HALF + i, :], ident[:])
+                nc.vector.tensor_tensor(
+                    out=res[:, m, cols], in0=scaled[:].rearrange("p i q -> p (i q)"), in1=x_sb[m][:, cols], op=ALU.add
+                )
+                if last and j == 0:
+                    nc.vector.tensor_reduce(
+                        out=res_padded[:, m, PAD + N : PAD + N + 1], in_=res_padded[:, m, PAD - 1 : PAD + HALF],
+                        axis=AX.X, op=ALU.max, apply_absolute_value=True,
+                    )
+                if last and j == 1:
+                    nc.vector.tensor_reduce(
+                        out=amax_part[:], in_=res_padded[:, m, PAD + HALF : PAD + N + 1], axis=AX.X, op=ALU.max, apply_absolute_value=True
+                    )
+            nc.sync.dma_start(out=out0_view[:, m, :], in_=res[:, m, 0:N])
+            if not last:
+                nc.vector.tensor_reduce(
+                    out=res_padded[:, m + 1, PAD - 1 : PAD], in_=res_padded[:, m, PAD - 1 : PAD + N],
+                    axis=AX.X, op=ALU.max, apply_absolute_value=True,
+                )
+
+        recip_part = sb.tile([P, 1], F32, name="rp")
+        nc.vector.reciprocal(out=recip_part[:], in_=amax_part[:])
+        recip_all = ps.tile([P, P], F32, name="bt", tag="bank")
+        nc.tensor.transpose(recip_all[:], recip_part[:, 0:1].to_broadcast([P, P]), ident[:])
+        factors = sb.tile([P, P], F32, name="scaled")
+        factor = sb.tile([P, 1], F32, name="fac")
         nc.vector.tensor_scalar(
-            out=scaled[:], in0=bt[:], scalar1=448.0, scalar2=None, op0=ALU.mult, op1=ALU.min, accum_out=fac[:]
+            out=factors[:], in0=recip_all[:], scalar1=FP8_MAX, scalar2=None, op0=ALU.mult, op1=ALU.min, accum_out=factor[:]
         )
 
-        for m in range(MT):
-            o8 = sb.tile([P, N], FP8, name="o8_%d" % m)
+        for m in range(TILES):
+            codes8 = sb.tile([P, N], FP8, name="o8_%d" % m)
             nc.vector.tensor_scalar(
-                out=o8[:, 0:V_CAST], in0=res[:, m, 0:V_CAST], scalar1=fac[:, 0:1], scalar2=None, op0=ALU.mult, saturate=False
+                out=codes8[:, 0:V_CAST], in0=res[:, m, 0:V_CAST], scalar1=factor[:, 0:1], scalar2=None, op0=ALU.mult, saturate=False
             )
             nc.scalar.activation(
-                out=o8[:, V_CAST:N], in_=res[:, m, V_CAST:N], func=ACT.Identity, scale=fac[:, 0:1], bias=zero[:, 0:1], saturate=False
+                out=codes8[:, V_CAST:N], in_=res[:, m, V_CAST:N], func=ACT.Identity, scale=factor[:, 0:1], bias=zero[:, 0:1], saturate=False
             )
-            nc.sync.dma_start(out=o1v[:, m, :], in_=o8[:].bitcast(U8))
+            nc.sync.dma_start(out=out1_view[:, m, :], in_=codes8[:].bitcast(U8))

@@ -32,7 +32,8 @@ FLOPS = 2 * TOKENS * K * N
 
 V_INTERLEAVE = 336
 V_CAST = 672
-V_NORMALISE = 2
+V_NORMALISE = 1
+PE_RESIDUAL = ((3, 0), (3, 1))
 
 
 def tile_dcadecoderblock_pb_kernel(tc, h_attn, x, attn_out_W, attn_out_b, attn_norm_g, attn_norm_b, out_0, out_1):
@@ -45,6 +46,7 @@ def tile_dcadecoderblock_pb_kernel(tc, h_attn, x, attn_out_W, attn_out_b, attn_n
     with ExitStack() as ctx:
         sb = ctx.enter_context(tc.tile_pool(name="sb", bufs=1))
         ps = ctx.enter_context(tc.psum_pool(name="ps", bufs=8))
+        ctx.enter_context(tc.manual_schedule())
 
         one = sb.tile([P, 1], F32, name="one")
         nc.vector.memset(one[:], 1.0)
@@ -82,13 +84,13 @@ def tile_dcadecoderblock_pb_kernel(tc, h_attn, x, attn_out_W, attn_out_b, attn_n
             x_sb[m] = t
 
         load_w(0, 0)
-        load_h(0)
-        load_h(1)
         for i, vec in enumerate((attn_norm_g, attn_norm_b, attn_out_b)):
             nc.sync.dma_start(out=rows[i * BLOCKS : (i + 1) * BLOCKS, :], in_=vec.rearrange("(c p) -> c p", p=P))
         load_w(1, 0)
+        load_h(0)
         load_w(0, 1)
         load_w(1, 1)
+        load_h(1)
         load_h(2)
         load_h(3)
         for m in range(TILES):
@@ -97,15 +99,21 @@ def tile_dcadecoderblock_pb_kernel(tc, h_attn, x, attn_out_W, attn_out_b, attn_n
         b_all = sb.tile([P, N], BF16, name="b_bc")
         gain_shift_cols = sb.tile([P, 2 * BLOCKS], F32, name="gb")
 
+        vec_ps = {}
+
         def lay_out_vectors():
             cols_ps = ps.tile([P, 2 * BLOCKS], F32, name="gbp", tag="bank")
             nc.tensor.matmul(out=cols_ps[:], lhsT=rows[:], rhs=ident16[:, 0 : 2 * BLOCKS], start=True, stop=True)
-            nc.vector.tensor_copy(out=gain_shift_cols[:], in_=cols_ps[:])
+            vec_ps["cols"] = cols_ps
             b_ps = ps.tile([P, BLOCKS, P], BF16, name="bb", tag="bank")
             for c in range(BLOCKS):
                 r = 2 * BLOCKS + c
                 nc.tensor.matmul(out=b_ps[:, c, :], lhsT=ident16[:, r : r + 1].to_broadcast([P, P]), rhs=rows[:], start=True, stop=True)
-            nc.scalar.copy(out=b_all[:], in_=b_ps[:].rearrange("p c q -> p (c q)"))
+            vec_ps["b"] = b_ps
+
+        def copy_vectors():
+            nc.vector.tensor_copy(out=gain_shift_cols[:], in_=vec_ps["cols"][:])
+            nc.scalar.copy(out=b_all[:], in_=vec_ps["b"][:].rearrange("p c q -> p (c q)"))
 
         w_grouped = {}
         w_codes = {}
@@ -173,123 +181,172 @@ def tile_dcadecoderblock_pb_kernel(tc, h_attn, x, attn_out_W, attn_out_b, attn_n
                 stop=(g == PASSES - 1),
             )
 
-        interleave_w(0, 0)
-        for m in (0, 1):
-            turn_h(m)
-            copy_h(m)
-        lay_out_vectors()
-        interleave_w(1, 0)
-        quantize_w(0, 0)
-        for m in (0, 1):
-            quantize_h(m)
-        for m in (0, 1):
-            mx(0, 0, m)
-        quantize_w(1, 0)
-        for m in (0, 1):
-            mx(1, 0, m)
-        interleave_w(0, 1)
-        interleave_w(1, 1)
-        for g in range(PASSES):
-            quantize_w(g, 1)
-            for m in (0, 1):
-                mx(g, 1, m)
-        for m in (2, 3):
-            turn_h(m)
-        for m in (2, 3):
-            copy_h(m)
-        for m in (2, 3):
-            quantize_h(m)
-        for m in (2, 3):
-            for j in range(HALVES):
-                for g in range(PASSES):
-                    mx(g, j, m)
-
-        squares_out = sb.tile([P, HALF], BF16, name="junk")
+        squares_out = sb.tile([P, N], BF16, name="junk")
         res_padded = sb.tile([P, TILES, PAD + N + PAD], F32, name="res")
         res = res_padded[:, :, PAD : PAD + N]
         amax_part = sb.tile([P, 1], F32, name="pm")
         nc.vector.memset(res_padded[:, 0, PAD - 1 : PAD], 0.0)
 
-        for m in range(TILES):
-            o = sb.tile([P, N], F32, name="o%d" % m)
-            sums = sb.tile([P, HALVES], F32, name="sums%d" % m)
-            ssq = sb.tile([P, HALVES], F32, name="ssq%d" % m)
-            neg_shift = sb.tile([P, 1], F32, name="negs%d" % m)
+        o_of = {}
+        sums_of = {}
+        neg_mean_of = {}
+        rstd_of = {}
+        shift_of = {}
+        normed_of = {}
+        normed_t_of = {}
+        scaled_t_of = {}
+        scaled_of = {}
 
-            def bias_add(j):
-                cols = slice(j * HALF, (j + 1) * HALF)
-                nc.vector.scalar_tensor_tensor(
-                    out=o[:, cols], in0=acc[(m, j)][:], scalar=1.0, in1=b_all[:, cols],
-                    op0=ALU.mult, op1=ALU.add, accum_out=sums[:, j : j + 1],
-                )
+        def bias_add(m, j):
+            if j == 0:
+                o_of[m] = sb.tile([P, N], F32, name="o%d" % m)
+                sums_of[m] = sb.tile([P, HALVES], F32, name="sums%d" % m)
+            cols = slice(j * HALF, (j + 1) * HALF)
+            nc.vector.scalar_tensor_tensor(
+                out=o_of[m][:, cols], in0=acc[(m, j)][:], scalar=1.0, in1=b_all[:, cols],
+                op0=ALU.mult, op1=ALU.add, accum_out=sums_of[m][:, j : j + 1],
+            )
 
-            def squares(j):
-                cols = slice(j * HALF, (j + 1) * HALF)
-                nc.scalar.activation(
-                    out=squares_out[:], in_=o[:, cols], func=ACT.Square, bias=neg_shift[:, 0:1], scale=1.0, accum_out=ssq[:, j : j + 1]
-                )
+        def mean(m):
+            neg_mean_of[m] = sb.tile([P, 1], F32, name="negmu%d" % m)
+            s = sums_of[m]
+            nc.vector.tensor_scalar(out=neg_mean_of[m][:], in0=s[:, 0:1], scalar1=s[:, 1:2], scalar2=-1.0 / N, op0=ALU.add, op1=ALU.mult)
 
-            bias_add(0)
-            nc.vector.tensor_scalar(out=neg_shift[:], in0=sums[:, 0:1], scalar1=-1.0 / HALF, scalar2=None, op0=ALU.mult)
-            squares(0)
-            bias_add(1)
-            squares(1)
-            s0 = sums[:, 0:1]
-            s1 = sums[:, 1:2]
-            neg_mean = sb.tile([P, 1], F32, name="negmu%d" % m)
-            d = sb.tile([P, 1], F32, name="d%d" % m)
-            nc.vector.tensor_scalar(out=d[:], in0=s1, scalar1=s0, scalar2=1.0 / N, op0=ALU.subtract, op1=ALU.mult)
-            nc.vector.tensor_scalar(out=neg_mean[:], in0=s0, scalar1=s1, scalar2=-1.0 / N, op0=ALU.add, op1=ALU.mult)
-            w = sb.tile([P, 1], F32, name="w%d" % m)
-            nc.vector.tensor_scalar(out=w[:], in0=d[:], scalar1=d[:, 0:1], scalar2=EPS, op0=ALU.mult, op1=ALU.subtract)
-            rest = sb.tile([P, 1], F32, name="vb%d" % m)
-            nc.vector.tensor_scalar(out=rest[:], in0=ssq[:, 0:1], scalar1=1.0 / N, scalar2=w[:, 0:1], op0=ALU.mult, op1=ALU.subtract)
-            rstd = sb.tile([P, 1], F32, name="rstd%d" % m)
-            nc.scalar.activation(out=rstd[:], in_=ssq[:, 1:2], func=ACT.Abs_reciprocal_sqrt, bias=rest[:, 0:1], scale=1.0 / N)
+        def deviation(m):
+            ssq = sb.tile([P, 1], F32, name="ssq%d" % m)
+            nc.scalar.activation(out=squares_out[:], in_=o_of[m][:], func=ACT.Square, bias=neg_mean_of[m][:, 0:1], scale=1.0, accum_out=ssq[:, 0:1])
+            rstd_of[m] = sb.tile([P, 1], F32, name="rstd%d" % m)
+            nc.scalar.activation(out=rstd_of[m][:], in_=ssq[:, 0:1], func=ACT.Abs_reciprocal_sqrt, bias=EPS, scale=1.0 / N)
+            shift_of[m] = sb.tile([P, 1], F32, name="shift%d" % m)
+            nc.scalar.activation(out=shift_of[m][:], in_=rstd_of[m][:], func=ACT.Copy, scale=neg_mean_of[m][:, 0:1])
 
-            normed = sb.tile([P, N], F32, name="nrm%d" % m)
-            scaled_t = sb.tile([P, BLOCKS, P], F32, name="yT%d" % m)
+        def normalise(m, j):
+            if j == 0:
+                normed_of[m] = sb.tile([P, N], F32, name="nrm%d" % m)
+            cols = slice(j * HALF, (j + 1) * HALF)
             engine = nc.vector if m < V_NORMALISE else nc.gpsimd
-            for j in range(HALVES):
-                cols = slice(j * HALF, (j + 1) * HALF)
-                engine.tensor_scalar(
-                    out=normed[:, cols], in0=o[:, cols], scalar1=neg_mean[:, 0:1], scalar2=rstd[:, 0:1], op0=ALU.add, op1=ALU.mult
+            engine.tensor_scalar(
+                out=normed_of[m][:, cols], in0=o_of[m][:, cols], scalar1=rstd_of[m][:, 0:1], scalar2=shift_of[m][:, 0:1], op0=ALU.mult, op1=ALU.add
+            )
+
+        def turn(m, j):
+            normed_t_of[(m, j)] = ps.tile([P, BLOCKS_PER_HALF, P], F32, name="nT%d%d" % (m, j), tag="bank")
+            for i in range(BLOCKS_PER_HALF):
+                c = j * BLOCKS_PER_HALF + i
+                nc.tensor.transpose(normed_t_of[(m, j)][:, i, :], normed_of[m][:, c * P : (c + 1) * P], ident[:])
+
+        def gain_shift(m, j):
+            if j == 0:
+                scaled_t_of[m] = sb.tile([P, BLOCKS, P], F32, name="yT%d" % m)
+            for i in range(BLOCKS_PER_HALF):
+                c = j * BLOCKS_PER_HALF + i
+                nc.scalar.activation(
+                    out=scaled_t_of[m][:, c, :], in_=normed_t_of[(m, j)][:, i, :], func=ACT.Identity,
+                    scale=gain_shift_cols[:, c : c + 1], bias=gain_shift_cols[:, BLOCKS + c : BLOCKS + c + 1],
                 )
-            for j in range(HALVES):
-                normed_t = ps.tile([P, BLOCKS_PER_HALF, P], F32, name="nT%d%d" % (m, j), tag="bank")
+
+        def turn_back(m, j):
+            cols = slice(j * HALF, (j + 1) * HALF)
+            scaled = ps.tile([P, BLOCKS_PER_HALF, P], F32, name="y%d%d" % (m, j), tag="bank")
+            scaled_of[(m, j)] = scaled
+            if (m, j) in PE_RESIDUAL:
+                nc.tensor.matmul(out=scaled[:].rearrange("p i q -> p (i q)"), lhsT=ident16[:], rhs=x_sb[m][:, cols], start=True, stop=False)
                 for i in range(BLOCKS_PER_HALF):
-                    c = j * BLOCKS_PER_HALF + i
-                    nc.tensor.transpose(normed_t[:, i, :], normed[:, c * P : (c + 1) * P], ident[:])
-                for i in range(BLOCKS_PER_HALF):
-                    c = j * BLOCKS_PER_HALF + i
-                    nc.scalar.activation(
-                        out=scaled_t[:, c, :], in_=normed_t[:, i, :], func=ACT.Identity,
-                        scale=gain_shift_cols[:, c : c + 1], bias=gain_shift_cols[:, BLOCKS + c : BLOCKS + c + 1],
+                    nc.tensor.matmul(
+                        out=scaled[:, i, :], lhsT=scaled_t_of[m][:, j * BLOCKS_PER_HALF + i, :], rhs=ident[:],
+                        is_transpose=True, start=False, stop=(i == BLOCKS_PER_HALF - 1),
                     )
+            else:
+                for i in range(BLOCKS_PER_HALF):
+                    nc.tensor.transpose(scaled[:, i, :], scaled_t_of[m][:, j * BLOCKS_PER_HALF + i, :], ident[:])
+
+        def residual(m, j):
+            cols = slice(j * HALF, (j + 1) * HALF)
+            flat = scaled_of[(m, j)][:].rearrange("p i q -> p (i q)")
+            if (m, j) in PE_RESIDUAL:
+                nc.scalar.copy(out=res[:, m, cols], in_=flat)
+            else:
+                nc.vector.tensor_tensor(out=res[:, m, cols], in0=flat, in1=x_sb[m][:, cols], op=ALU.add)
+
+        def largest(m, j):
             last = m == TILES - 1
-            for j in range(HALVES):
-                cols = slice(j * HALF, (j + 1) * HALF)
-                scaled = ps.tile([P, BLOCKS_PER_HALF, P], F32, name="y%d%d" % (m, j), tag="bank")
-                for i in range(BLOCKS_PER_HALF):
-                    nc.tensor.transpose(scaled[:, i, :], scaled_t[:, j * BLOCKS_PER_HALF + i, :], ident[:])
-                nc.vector.tensor_tensor(
-                    out=res[:, m, cols], in0=scaled[:].rearrange("p i q -> p (i q)"), in1=x_sb[m][:, cols], op=ALU.add
-                )
-                if last and j == 0:
-                    nc.vector.tensor_reduce(
-                        out=res_padded[:, m, PAD + N : PAD + N + 1], in_=res_padded[:, m, PAD - 1 : PAD + HALF],
-                        axis=AX.X, op=ALU.max, apply_absolute_value=True,
-                    )
-                if last and j == 1:
-                    nc.vector.tensor_reduce(
-                        out=amax_part[:], in_=res_padded[:, m, PAD + HALF : PAD + N + 1], axis=AX.X, op=ALU.max, apply_absolute_value=True
-                    )
-            nc.sync.dma_start(out=out0_view[:, m, :], in_=res[:, m, 0:N])
-            if not last:
+            if not last and j == 1:
                 nc.vector.tensor_reduce(
                     out=res_padded[:, m + 1, PAD - 1 : PAD], in_=res_padded[:, m, PAD - 1 : PAD + N],
                     axis=AX.X, op=ALU.max, apply_absolute_value=True,
                 )
+            if last and j == 0:
+                nc.vector.tensor_reduce(
+                    out=res_padded[:, m, PAD + N : PAD + N + 1], in_=res_padded[:, m, PAD - 1 : PAD + HALF],
+                    axis=AX.X, op=ALU.max, apply_absolute_value=True,
+                )
+            if last and j == 1:
+                nc.vector.tensor_reduce(
+                    out=amax_part[:], in_=res_padded[:, m, PAD + HALF : PAD + N + 1], axis=AX.X, op=ALU.max, apply_absolute_value=True
+                )
+
+        def store(m):
+            nc.sync.dma_start(out=out0_view[:, m, :], in_=res[:, m, 0:N])
+
+        def mx_tile(m):
+            for j in range(HALVES):
+                for g in range(PASSES):
+                    mx(g, j, m)
+
+        interleave_w(0, 0)
+        interleave_w(1, 0)
+        lay_out_vectors()
+        copy_vectors()
+        turn_h(0)
+        copy_h(0)
+        quantize_w(0, 0)
+        quantize_w(1, 0)
+        interleave_w(0, 1)
+        quantize_h(0)
+        mx(0, 0, 0)
+        mx(1, 0, 0)
+        interleave_w(1, 1)
+        quantize_w(0, 1)
+        quantize_w(1, 1)
+        for m in (1, 2, 3):
+            turn_h(m)
+            copy_h(m)
+        mx(0, 1, 0)
+        mx(1, 1, 0)
+        bias_add(0, 0)
+        quantize_h(1)
+        mx_tile(1)
+        bias_add(0, 1)
+        mean(0)
+        deviation(0)
+        quantize_h(2)
+        mx_tile(2)
+        bias_add(1, 0)
+        bias_add(1, 1)
+        mean(1)
+        deviation(1)
+        quantize_h(3)
+        for j in range(HALVES):
+            normalise(0, j)
+            turn(0, j)
+        mx_tile(3)
+        for m in (2, 3):
+            bias_add(m, 0)
+            bias_add(m, 1)
+            mean(m)
+        for m in range(TILES):
+            for j in range(HALVES):
+                gain_shift(m, j)
+                turn_back(m, j)
+                if m + 1 < TILES:
+                    normalise(m + 1, j)
+                    turn(m + 1, j)
+            if m + 2 < TILES:
+                deviation(m + 2)
+            for j in range(HALVES):
+                residual(m, j)
+                largest(m, j)
+            store(m)
 
         recip_part = sb.tile([P, 1], F32, name="rp")
         nc.vector.reciprocal(out=recip_part[:], in_=amax_part[:])

@@ -112,7 +112,7 @@ def tile_dcadecoderblock_pb_kernel(tc, h_attn, x, attn_out_W, attn_out_b, attn_n
             vec_ps["b"] = b_ps
 
         def copy_vectors():
-            nc.vector.tensor_copy(out=gain_shift_cols[:], in_=vec_ps["cols"][:])
+            nc.scalar.copy(out=gain_shift_cols[:], in_=vec_ps["cols"][:])
             nc.scalar.copy(out=b_all[:], in_=vec_ps["b"][:].rearrange("p c q -> p (c q)"))
 
         w_grouped = {}
@@ -187,11 +187,11 @@ def tile_dcadecoderblock_pb_kernel(tc, h_attn, x, attn_out_W, attn_out_b, attn_n
         amax_part = sb.tile([P, 1], F32, name="pm")
         nc.vector.memset(res_padded[:, 0, PAD - 1 : PAD], 0.0)
 
+        scaled_sums = sb.tile([P, HALVES], F32, name="ssums")
         o_of = {}
         sums_of = {}
         neg_mean_of = {}
         rstd_of = {}
-        shift_of = {}
         normed_of = {}
         normed_t_of = {}
         scaled_t_of = {}
@@ -210,15 +210,14 @@ def tile_dcadecoderblock_pb_kernel(tc, h_attn, x, attn_out_W, attn_out_b, attn_n
         def mean(m):
             neg_mean_of[m] = sb.tile([P, 1], F32, name="negmu%d" % m)
             s = sums_of[m]
-            nc.vector.tensor_scalar(out=neg_mean_of[m][:], in0=s[:, 0:1], scalar1=s[:, 1:2], scalar2=-1.0 / N, op0=ALU.add, op1=ALU.mult)
+            nc.scalar.activation(out=scaled_sums[:], in_=s[:], func=ACT.Copy, scale=-1.0 / N, accum_out=neg_mean_of[m][:, 0:1])
 
         def deviation(m):
+            mean(m)
             ssq = sb.tile([P, 1], F32, name="ssq%d" % m)
             nc.scalar.activation(out=squares_out[:], in_=o_of[m][:], func=ACT.Square, bias=neg_mean_of[m][:, 0:1], scale=1.0, accum_out=ssq[:, 0:1])
             rstd_of[m] = sb.tile([P, 1], F32, name="rstd%d" % m)
             nc.scalar.activation(out=rstd_of[m][:], in_=ssq[:, 0:1], func=ACT.Abs_reciprocal_sqrt, bias=EPS, scale=1.0 / N)
-            shift_of[m] = sb.tile([P, 1], F32, name="shift%d" % m)
-            nc.scalar.activation(out=shift_of[m][:], in_=rstd_of[m][:], func=ACT.Copy, scale=neg_mean_of[m][:, 0:1])
 
         def normalise(m, j):
             if j == 0:
@@ -226,7 +225,7 @@ def tile_dcadecoderblock_pb_kernel(tc, h_attn, x, attn_out_W, attn_out_b, attn_n
             cols = slice(j * HALF, (j + 1) * HALF)
             engine = nc.vector if m < V_NORMALISE else nc.gpsimd
             engine.tensor_scalar(
-                out=normed_of[m][:, cols], in0=o_of[m][:, cols], scalar1=rstd_of[m][:, 0:1], scalar2=shift_of[m][:, 0:1], op0=ALU.mult, op1=ALU.add
+                out=normed_of[m][:, cols], in0=o_of[m][:, cols], scalar1=neg_mean_of[m][:, 0:1], scalar2=rstd_of[m][:, 0:1], op0=ALU.add, op1=ALU.mult
             )
 
         def turn(m, j):
@@ -245,12 +244,17 @@ def tile_dcadecoderblock_pb_kernel(tc, h_attn, x, attn_out_W, attn_out_b, attn_n
                     scale=gain_shift_cols[:, c : c + 1], bias=gain_shift_cols[:, BLOCKS + c : BLOCKS + c + 1],
                 )
 
-        def turn_back(m, j):
+        def lay_residual(m, j):
             cols = slice(j * HALF, (j + 1) * HALF)
             scaled = ps.tile([P, BLOCKS_PER_HALF, P], F32, name="y%d%d" % (m, j), tag="bank")
             scaled_of[(m, j)] = scaled
+            nc.tensor.matmul(out=scaled[:].rearrange("p i q -> p (i q)"), lhsT=ident16[:], rhs=x_sb[m][:, cols], start=True, stop=False)
+
+        def turn_back(m, j):
+            if (m, j) not in PE_RESIDUAL:
+                scaled_of[(m, j)] = ps.tile([P, BLOCKS_PER_HALF, P], F32, name="y%d%d" % (m, j), tag="bank")
+            scaled = scaled_of[(m, j)]
             if (m, j) in PE_RESIDUAL:
-                nc.tensor.matmul(out=scaled[:].rearrange("p i q -> p (i q)"), lhsT=ident16[:], rhs=x_sb[m][:, cols], start=True, stop=False)
                 for i in range(BLOCKS_PER_HALF):
                     nc.tensor.matmul(
                         out=scaled[:, i, :], lhsT=scaled_t_of[m][:, j * BLOCKS_PER_HALF + i, :], rhs=ident[:],
@@ -317,13 +321,11 @@ def tile_dcadecoderblock_pb_kernel(tc, h_attn, x, attn_out_W, attn_out_b, attn_n
         quantize_h(1)
         mx_tile(1)
         bias_add(0, 1)
-        mean(0)
         deviation(0)
         quantize_h(2)
         mx_tile(2)
         bias_add(1, 0)
         bias_add(1, 1)
-        mean(1)
         deviation(1)
         quantize_h(3)
         for j in range(HALVES):
@@ -333,7 +335,6 @@ def tile_dcadecoderblock_pb_kernel(tc, h_attn, x, attn_out_W, attn_out_b, attn_n
         for m in (2, 3):
             bias_add(m, 0)
             bias_add(m, 1)
-            mean(m)
         for m in range(TILES):
             for j in range(HALVES):
                 gain_shift(m, j)
@@ -341,6 +342,9 @@ def tile_dcadecoderblock_pb_kernel(tc, h_attn, x, attn_out_W, attn_out_b, attn_n
                 if m + 1 < TILES:
                     normalise(m + 1, j)
                     turn(m + 1, j)
+            if m == 1:
+                for mj in PE_RESIDUAL:
+                    lay_residual(mj[0], mj[1])
             if m + 2 < TILES:
                 deviation(m + 2)
             for j in range(HALVES):

@@ -33,6 +33,7 @@ FLOPS = 2 * TOKENS * K * N
 V_INTERLEAVE = 336
 V_CAST = 672
 V_NORMALISE = 1
+S_MEANS = 2
 PE_RESIDUAL = ((3, 0), (3, 1))
 
 
@@ -185,7 +186,6 @@ def tile_dcadecoderblock_pb_kernel(tc, h_attn, x, attn_out_W, attn_out_b, attn_n
         res_padded = sb.tile([P, TILES, PAD + N + PAD], F32, name="res")
         res = res_padded[:, :, PAD : PAD + N]
         amax_part = sb.tile([P, 1], F32, name="pm")
-        nc.vector.memset(res_padded[:, 0, PAD - 1 : PAD], 0.0)
 
         scaled_sums = sb.tile([P, HALVES], F32, name="ssums")
         o_of = {}
@@ -210,10 +210,16 @@ def tile_dcadecoderblock_pb_kernel(tc, h_attn, x, attn_out_W, attn_out_b, attn_n
         def mean(m):
             neg_mean_of[m] = sb.tile([P, 1], F32, name="negmu%d" % m)
             s = sums_of[m]
-            nc.scalar.activation(out=scaled_sums[:], in_=s[:], func=ACT.Copy, scale=-1.0 / N, accum_out=neg_mean_of[m][:, 0:1])
+            if m < S_MEANS:
+                nc.scalar.activation(out=scaled_sums[:], in_=s[:], func=ACT.Copy, scale=-1.0 / N, accum_out=neg_mean_of[m][:, 0:1])
+            else:
+                nc.vector.tensor_scalar(
+                    out=neg_mean_of[m][:], in0=s[:, 0:1], scalar1=s[:, 1:2], scalar2=-1.0 / N, op0=ALU.add, op1=ALU.mult
+                )
 
         def deviation(m):
-            mean(m)
+            if m < S_MEANS:
+                mean(m)
             ssq = sb.tile([P, 1], F32, name="ssq%d" % m)
             nc.scalar.activation(out=squares_out[:], in_=o_of[m][:], func=ACT.Square, bias=neg_mean_of[m][:, 0:1], scale=1.0, accum_out=ssq[:, 0:1])
             rstd_of[m] = sb.tile([P, 1], F32, name="rstd%d" % m)
@@ -273,21 +279,14 @@ def tile_dcadecoderblock_pb_kernel(tc, h_attn, x, attn_out_W, attn_out_b, attn_n
                 nc.vector.tensor_tensor(out=res[:, m, cols], in0=flat, in1=x_sb[m][:, cols], op=ALU.add)
 
         def largest(m, j):
-            last = m == TILES - 1
-            if not last and j == 1:
-                nc.vector.tensor_reduce(
-                    out=res_padded[:, m + 1, PAD - 1 : PAD], in_=res_padded[:, m, PAD - 1 : PAD + N],
-                    axis=AX.X, op=ALU.max, apply_absolute_value=True,
-                )
-            if last and j == 0:
-                nc.vector.tensor_reduce(
-                    out=res_padded[:, m, PAD + N : PAD + N + 1], in_=res_padded[:, m, PAD - 1 : PAD + HALF],
-                    axis=AX.X, op=ALU.max, apply_absolute_value=True,
-                )
-            if last and j == 1:
-                nc.vector.tensor_reduce(
-                    out=amax_part[:], in_=res_padded[:, m, PAD + HALF : PAD + N + 1], axis=AX.X, op=ALU.max, apply_absolute_value=True
-                )
+            piece = m * HALVES + j
+            half = res_padded[:, m, PAD + j * HALF : PAD + (j + 1) * HALF]
+            if piece < TILES * HALVES - 1:
+                out = res_padded[:, TILES - 1, PAD + N + piece : PAD + N + piece + 1]
+            else:
+                out = amax_part[:]
+                half = res_padded[:, m, PAD + j * HALF : PAD + N + piece]
+            nc.vector.tensor_reduce(out=out, in_=half, axis=AX.X, op=ALU.max, apply_absolute_value=True)
 
         def store(m):
             nc.sync.dma_start(out=out0_view[:, m, :], in_=res[:, m, 0:N])
@@ -335,6 +334,7 @@ def tile_dcadecoderblock_pb_kernel(tc, h_attn, x, attn_out_W, attn_out_b, attn_n
         for m in (2, 3):
             bias_add(m, 0)
             bias_add(m, 1)
+            mean(m)
         for m in range(TILES):
             for j in range(HALVES):
                 gain_shift(m, j)
@@ -349,6 +349,7 @@ def tile_dcadecoderblock_pb_kernel(tc, h_attn, x, attn_out_W, attn_out_b, attn_n
                 deviation(m + 2)
             for j in range(HALVES):
                 residual(m, j)
+            for j in range(HALVES):
                 largest(m, j)
             store(m)
 

from contextlib import ExitStack

import concourse.masks as masks
import concourse.mybir as mybir

F32 = mybir.dt.float32
BF16 = mybir.dt.bfloat16
U32 = mybir.dt.uint32
U8 = mybir.dt.uint8
FP8X4 = mybir.dt.float8_e4m3fn_x4
FP8 = mybir.dt.float8_e4m3fn
ALU = mybir.AluOpType
ACT = mybir.ActivationFunctionType
AX = mybir.AxisListType

P = 128
TOKENS = 512
K = 1024
N = 1024
TILES = TOKENS // P
PACK = 4
K_PASS = P * PACK
PASSES = K // K_PASS
HALF = 512
HALVES = N // HALF
BLOCKS = N // P
BLOCKS_PER_HALF = HALF // P
EPS = 1e-5
FP8_MAX = 448.0
PAD = 8
FLOPS = 2 * TOKENS * K * N

V_INTERLEAVE = 336
V_CAST = 672
V_NORMALISE = 1
S_MEANS = 2
PE_RESIDUAL = ((3, 0), (3, 1))


def tile_dcadecoderblock_pb_kernel(tc, h_attn, x, attn_out_W, attn_out_b, attn_norm_g, attn_norm_b, out_0, out_1):
    nc = tc.nc
    h_view = h_attn.flatten_outer_dims().rearrange("(p m) k -> p m k", m=TILES)
    x_view = x.flatten_outer_dims().rearrange("(p m) n -> p m n", m=TILES)
    out0_view = out_0.flatten_outer_dims().rearrange("(p m) n -> p m n", m=TILES)
    out1_view = out_1.flatten_outer_dims().rearrange("(p m) n -> p m n", m=TILES)

    with ExitStack() as ctx:
        sb = ctx.enter_context(tc.tile_pool(name="sb", bufs=1))
        ps = ctx.enter_context(tc.psum_pool(name="ps", bufs=8))
        ctx.enter_context(tc.manual_schedule())

        one = sb.tile([P, 1], F32, name="one")
        nc.vector.memset(one[:], 1.0)
        zero = sb.tile([P, 1], F32, name="zero")
        nc.vector.memset(zero[:], 0.0)
        rows = sb.tile([P, P], BF16, name="rows")
        nc.vector.memset(rows[:].bitcast(F32), 0.0)
        warm = sb.tile([P, 1], F32, name="warm")
        nc.scalar.activation(out=warm[:], in_=one[:], func=ACT.Abs_reciprocal_sqrt)
        ident = sb.tile([P, P], F32, name="ident")
        masks.make_identity(nc, ident[:])
        ident16 = sb.tile([P, P], BF16, name="ident16")
        nc.vector.tensor_copy(out=ident16[:], in_=ident[:])

        w_raw = {}
        h_sb = {}
        x_sb = {}

        def load_w(g, j):
            t = sb.tile([P, PACK, HALF], BF16, name="wraw%d%d" % (g, j))
            nc.sync.dma_start(
                out=t[:],
                in_=attn_out_W[g * K_PASS : (g + 1) * K_PASS, j * HALF : (j + 1) * HALF].rearrange("(p t) n -> p t n", t=PACK),
            )
            w_raw[(g, j)] = t

        def load_h(m):
            t = sb.tile([P, K], BF16, name="hsb%d" % m)
            nc.sync.dma_start(out=t[:], in_=h_view[:, m, :])
            h_sb[m] = t

        def load_x(m):
            t = sb.tile([P, N], BF16, name="xsb%d" % m)
            nc.sync.dma_start(out=t[:], in_=x_view[:, m, :])
            x_sb[m] = t

        load_w(0, 0)
        for i, vec in enumerate((attn_norm_g, attn_norm_b, attn_out_b)):
            nc.sync.dma_start(out=rows[i * BLOCKS : (i + 1) * BLOCKS, :], in_=vec.rearrange("(c p) -> c p", p=P))
        load_w(1, 0)
        load_h(0)
        load_w(0, 1)
        load_w(1, 1)
        load_h(1)
        load_h(2)
        load_h(3)
        for m in range(TILES):
            load_x(m)

        b_all = sb.tile([P, N], BF16, name="b_bc")
        gain_shift_cols = sb.tile([P, 2 * BLOCKS], F32, name="gb")

        vec_ps = {}

        def lay_out_vectors():
            cols_ps = ps.tile([P, 2 * BLOCKS], F32, name="gbp", tag="bank")
            nc.tensor.matmul(out=cols_ps[:], lhsT=rows[:], rhs=ident16[:, 0 : 2 * BLOCKS], start=True, stop=True)
            vec_ps["cols"] = cols_ps
            b_ps = ps.tile([P, BLOCKS, P], BF16, name="bb", tag="bank")
            for c in range(BLOCKS):
                r = 2 * BLOCKS + c
                nc.tensor.matmul(out=b_ps[:, c, :], lhsT=ident16[:, r : r + 1].to_broadcast([P, P]), rhs=rows[:], start=True, stop=True)
            vec_ps["b"] = b_ps

        def copy_vectors():
            nc.scalar.copy(out=gain_shift_cols[:], in_=vec_ps["cols"][:])
            nc.scalar.copy(out=b_all[:], in_=vec_ps["b"][:].rearrange("p c q -> p (c q)"))

        w_grouped = {}
        w_codes = {}
        w_scales = {}
        h_turned = {}
        h_grouped = {}
        h_codes = {}
        h_scales = {}
        acc = {}

        def interleave_w(g, j):
            grouped = sb.tile([P, HALF * PACK], BF16, name="wgrp%d%d" % (g, j), align_bytes=64)
            dst = grouped[:].rearrange("p (n t) -> p n t", t=PACK)
            raw = w_raw[(g, j)]
            nc.vector.tensor_copy(
                out=dst[:, 0:V_INTERLEAVE, :].rearrange("p (c i) t -> p c t i", i=4),
                in_=raw[:, :, 0:V_INTERLEAVE].rearrange("p t (c i) -> p c t i", i=4),
            )
            nc.scalar.copy(
                out=dst[:, V_INTERLEAVE:HALF, :].rearrange("p (c i) t -> p c t i", i=4),
                in_=raw[:, :, V_INTERLEAVE:HALF].rearrange("p t (c i) -> p c t i", i=4),
            )
            w_grouped[(g, j)] = grouped

        def quantize_w(g, j):
            codes = sb.tile([P, HALF], U32, name="wc%d%d" % (g, j), align_bytes=64)
            scales = sb.tile([P, HALF], U8, name="ws%d%d" % (g, j), align_bytes=64)
            nc.vector.quantize_mx(out=codes[:].bitcast(FP8X4), scales=scales[:], in_=w_grouped[(g, j)][:])
            w_codes[(g, j)] = codes
            w_scales[(g, j)] = scales

        def turn_h(m):
            words = h_sb[m][:].bitcast(F32)
            turned = ps.tile([P, PASSES, 2, P], F32, name="xt%d" % m, tag="bank")
            for g in range(PASSES):
                for u in range(2):
                    nc.tensor.transpose(turned[:, g, u, :], words[:, 256 * g + u : 256 * (g + 1) : 2], ident[:])
            h_turned[m] = turned

        def copy_h(m):
            grouped = sb.tile([P, PASSES * P * PACK], BF16, name="hgrp%d" % m, align_bytes=64)
            nc.scalar.copy(
                out=grouped[:].bitcast(F32).rearrange("p (g r u) -> p g r u", g=PASSES, u=2),
                in_=h_turned[m][:].rearrange("p g u r -> p g r u"),
            )
            h_grouped[m] = grouped

        def quantize_h(m):
            codes = sb.tile([P, PASSES * P], U32, name="hc%d" % m, align_bytes=64)
            scales = sb.tile([P, PASSES * P], U8, name="hs%d" % m, align_bytes=64)
            nc.vector.quantize_mx(out=codes[:].bitcast(FP8X4), scales=scales[:], in_=h_grouped[m][:])
            h_codes[m] = codes
            h_scales[m] = scales

        def mx(g, j, m):
            if g == 0:
                acc[(m, j)] = ps.tile([P, HALF], F32, name="acc%d%d" % (m, j), tag="bank")
            nc.tensor.matmul_mx(
                out=acc[(m, j)][:],
                lhsT=h_codes[m][:, g * P : (g + 1) * P].bitcast(FP8X4),
                lhsT_scale=h_scales[m][:, g * P : (g + 1) * P],
                rhs=w_codes[(g, j)][:].bitcast(FP8X4),
                rhs_scale=w_scales[(g, j)][:],
                start=(g == 0),
                stop=(g == PASSES - 1),
            )

        squares_out = sb.tile([P, N], BF16, name="junk")
        res_padded = sb.tile([P, TILES, PAD + N + PAD], F32, name="res")
        res = res_padded[:, :, PAD : PAD + N]
        amax_part = sb.tile([P, 1], F32, name="pm")

        scaled_sums = sb.tile([P, HALVES], F32, name="ssums")
        o_of = {}
        sums_of = {}
        neg_mean_of = {}
        rstd_of = {}
        normed_of = {}
        normed_t_of = {}
        scaled_t_of = {}
        scaled_of = {}

        def bias_add(m, j):
            if j == 0:
                o_of[m] = sb.tile([P, N], F32, name="o%d" % m)
                sums_of[m] = sb.tile([P, HALVES], F32, name="sums%d" % m)
            cols = slice(j * HALF, (j + 1) * HALF)
            nc.vector.scalar_tensor_tensor(
                out=o_of[m][:, cols], in0=acc[(m, j)][:], scalar=1.0, in1=b_all[:, cols],
                op0=ALU.mult, op1=ALU.add, accum_out=sums_of[m][:, j : j + 1],
            )

        def mean(m):
            neg_mean_of[m] = sb.tile([P, 1], F32, name="negmu%d" % m)
            s = sums_of[m]
            if m < S_MEANS:
                nc.scalar.activation(out=scaled_sums[:], in_=s[:], func=ACT.Copy, scale=-1.0 / N, accum_out=neg_mean_of[m][:, 0:1])
            else:
                nc.vector.tensor_scalar(
                    out=neg_mean_of[m][:], in0=s[:, 0:1], scalar1=s[:, 1:2], scalar2=-1.0 / N, op0=ALU.add, op1=ALU.mult
                )

        def deviation(m):
            if m < S_MEANS:
                mean(m)
            ssq = sb.tile([P, 1], F32, name="ssq%d" % m)
            nc.scalar.activation(out=squares_out[:], in_=o_of[m][:], func=ACT.Square, bias=neg_mean_of[m][:, 0:1], scale=1.0, accum_out=ssq[:, 0:1])
            rstd_of[m] = sb.tile([P, 1], F32, name="rstd%d" % m)
            nc.scalar.activation(out=rstd_of[m][:], in_=ssq[:, 0:1], func=ACT.Abs_reciprocal_sqrt, bias=EPS, scale=1.0 / N)

        def normalise(m, j):
            if j == 0:
                normed_of[m] = sb.tile([P, N], F32, name="nrm%d" % m)
            cols = slice(j * HALF, (j + 1) * HALF)
            engine = nc.vector if m < V_NORMALISE else nc.gpsimd
            engine.tensor_scalar(
                out=normed_of[m][:, cols], in0=o_of[m][:, cols], scalar1=neg_mean_of[m][:, 0:1], scalar2=rstd_of[m][:, 0:1], op0=ALU.add, op1=ALU.mult
            )

        def turn(m, j):
            normed_t_of[(m, j)] = ps.tile([P, BLOCKS_PER_HALF, P], F32, name="nT%d%d" % (m, j), tag="bank")
            for i in range(BLOCKS_PER_HALF):
                c = j * BLOCKS_PER_HALF + i
                nc.tensor.transpose(normed_t_of[(m, j)][:, i, :], normed_of[m][:, c * P : (c + 1) * P], ident[:])

        def gain_shift(m, j):
            if j == 0:
                scaled_t_of[m] = sb.tile([P, BLOCKS, P], F32, name="yT%d" % m)
            for i in range(BLOCKS_PER_HALF):
                c = j * BLOCKS_PER_HALF + i
                nc.scalar.activation(
                    out=scaled_t_of[m][:, c, :], in_=normed_t_of[(m, j)][:, i, :], func=ACT.Identity,
                    scale=gain_shift_cols[:, c : c + 1], bias=gain_shift_cols[:, BLOCKS + c : BLOCKS + c + 1],
                )

        def lay_residual(m, j):
            cols = slice(j * HALF, (j + 1) * HALF)
            scaled = ps.tile([P, BLOCKS_PER_HALF, P], F32, name="y%d%d" % (m, j), tag="bank")
            scaled_of[(m, j)] = scaled
            nc.tensor.matmul(out=scaled[:].rearrange("p i q -> p (i q)"), lhsT=ident16[:], rhs=x_sb[m][:, cols], start=True, stop=False)

        def turn_back(m, j):
            if (m, j) not in PE_RESIDUAL:
                scaled_of[(m, j)] = ps.tile([P, BLOCKS_PER_HALF, P], F32, name="y%d%d" % (m, j), tag="bank")
            scaled = scaled_of[(m, j)]
            if (m, j) in PE_RESIDUAL:
                for i in range(BLOCKS_PER_HALF):
                    nc.tensor.matmul(
                        out=scaled[:, i, :], lhsT=scaled_t_of[m][:, j * BLOCKS_PER_HALF + i, :], rhs=ident[:],
                        is_transpose=True, start=False, stop=(i == BLOCKS_PER_HALF - 1),
                    )
            else:
                for i in range(BLOCKS_PER_HALF):
                    nc.tensor.transpose(scaled[:, i, :], scaled_t_of[m][:, j * BLOCKS_PER_HALF + i, :], ident[:])

        def residual(m, j):
            cols = slice(j * HALF, (j + 1) * HALF)
            flat = scaled_of[(m, j)][:].rearrange("p i q -> p (i q)")
            if (m, j) in PE_RESIDUAL:
                nc.scalar.copy(out=res[:, m, cols], in_=flat)
            else:
                nc.vector.tensor_tensor(out=res[:, m, cols], in0=flat, in1=x_sb[m][:, cols], op=ALU.add)

        def largest(m, j):
            piece = m * HALVES + j
            half = res_padded[:, m, PAD + j * HALF : PAD + (j + 1) * HALF]
            if piece < TILES * HALVES - 1:
                out = res_padded[:, TILES - 1, PAD + N + piece : PAD + N + piece + 1]
            else:
                out = amax_part[:]
                half = res_padded[:, m, PAD + j * HALF : PAD + N + piece]
            nc.vector.tensor_reduce(out=out, in_=half, axis=AX.X, op=ALU.max, apply_absolute_value=True)

        def store(m):
            nc.sync.dma_start(out=out0_view[:, m, :], in_=res[:, m, 0:N])

        def mx_tile(m):
            for j in range(HALVES):
                for g in range(PASSES):
                    mx(g, j, m)

        interleave_w(0, 0)
        interleave_w(1, 0)
        lay_out_vectors()
        copy_vectors()
        turn_h(0)
        copy_h(0)
        quantize_w(0, 0)
        quantize_w(1, 0)
        interleave_w(0, 1)
        quantize_h(0)
        mx(0, 0, 0)
        mx(1, 0, 0)
        interleave_w(1, 1)
        quantize_w(0, 1)
        quantize_w(1, 1)
        for m in (1, 2, 3):
            turn_h(m)
            copy_h(m)
        mx(0, 1, 0)
        mx(1, 1, 0)
        bias_add(0, 0)
        quantize_h(1)
        mx_tile(1)
        bias_add(0, 1)
        deviation(0)
        quantize_h(2)
        mx_tile(2)
        bias_add(1, 0)
        bias_add(1, 1)
        deviation(1)
        quantize_h(3)
        for j in range(HALVES):
            normalise(0, j)
            turn(0, j)
        mx_tile(3)
        for m in (2, 3):
            bias_add(m, 0)
            bias_add(m, 1)
            mean(m)
        for m in range(TILES):
            for j in range(HALVES):
                gain_shift(m, j)
                turn_back(m, j)
                if m + 1 < TILES:
                    normalise(m + 1, j)
                    turn(m + 1, j)
            if m == 1:
                for mj in PE_RESIDUAL:
                    lay_residual(mj[0], mj[1])
            if m + 2 < TILES:
                deviation(m + 2)
            for j in range(HALVES):
                residual(m, j)
            for j in range(HALVES):
                largest(m, j)
            store(m)

        recip_part = sb.tile([P, 1], F32, name="rp")
        nc.vector.reciprocal(out=recip_part[:], in_=amax_part[:])
        recip_all = ps.tile([P, P], F32, name="bt", tag="bank")
        nc.tensor.transpose(recip_all[:], recip_part[:, 0:1].to_broadcast([P, P]), ident[:])
        factors = sb.tile([P, P], F32, name="scaled")
        factor = sb.tile([P, 1], F32, name="fac")
        nc.vector.tensor_scalar(
            out=factors[:], in0=recip_all[:], scalar1=FP8_MAX, scalar2=None, op0=ALU.mult, op1=ALU.min, accum_out=factor[:]
        )

        for m in range(TILES):
            codes8 = sb.tile([P, N], FP8, name="o8_%d" % m)
            nc.vector.tensor_scalar(
                out=codes8[:, 0:V_CAST], in0=res[:, m, 0:V_CAST], scalar1=factor[:, 0:1], scalar2=None, op0=ALU.mult, saturate=False
            )
            nc.scalar.activation(
                out=codes8[:, V_CAST:N], in_=res[:, m, V_CAST:N], func=ACT.Identity, scale=factor[:, 0:1], bias=zero[:, 0:1], saturate=False
            )
            nc.sync.dma_start(out=out1_view[:, m, :], in_=codes8[:].bitcast(U8))
